import numpy as np
import ml_dtypes


def mxq(x, axis, fmt="e4m3"):
    dtype, down = {"e4m3": (ml_dtypes.float8_e4m3fn, 7), "e5m2": (ml_dtypes.float8_e5m2, 14)}[fmt]
    v = np.moveaxis(np.asarray(x, np.float32).astype(ml_dtypes.bfloat16).astype(np.float64), axis, -1)
    blocks = v.reshape(v.shape[:-1] + (-1, 32))
    amax = np.abs(blocks).max(-1, keepdims=True)
    byte = np.maximum(np.where(amax > 0, np.frexp(amax)[1] - 1 + 127, 0) - down, 1)
    scale = np.exp2(byte - 127.0)
    codes = (blocks / scale).astype(np.float32).astype(dtype).astype(np.float64)
    return np.moveaxis((codes * scale).reshape(v.shape), -1, axis)


WIDE = False


def mx_kscale(k):
    if not WIDE:
        return np.ones(k)
    levels = np.array([10, -10, 5, -5, 0])
    a = np.random.permutation(np.resize(levels, k // 512 * 4)).reshape(k // 512, 4)
    idx = np.arange(k)
    return np.exp2(a[idx // 512, idx % 128 // 32])


BF16 = ml_dtypes.bfloat16


def bf(x):
    return np.asarray(x, np.float32).astype(BF16)


def f64(x):
    return np.asarray(x).astype(np.float64)


B, T, D, NH, HD, G, RD, F = 2, 2048, 1024, 8, 128, 2, 16, 512
LN_SCALE = 1.0 / np.sqrt(12.0)
EPS_RMS = 1e-6


def rmsnorm(x, eps):
    return x / np.sqrt(np.mean(np.square(x), axis=-1, keepdims=True) + eps)


def setup_inputs():
    t = np.exp2(np.round(np.log2(mx_kscale(F)) / 2))
    return {"x_mid": bf(np.random.standard_normal((B, T, D)) * np.random.uniform(0.5, 2.0, (B, T, 1))),
            "wfc": bf(np.random.standard_normal((F, D)) / (LN_SCALE * np.sqrt(D)) * t[:, None]),
            "wproj": bf(np.random.standard_normal((D, F)) / np.sqrt(F) / (t * t)[None, :]),
            "mlp_scale": bf(1.0 + 0.1 * np.random.standard_normal(D))}


def reference(x_mid, wfc, wproj, mlp_scale):
    x = f64(x_mid)
    h2 = rmsnorm(x, EPS_RMS) * LN_SCALE
    u = mxq(h2, 2, "e4m3") @ mxq(f64(wfc), 1, "e4m3").T
    act = np.square(np.where(u >= 0, u, 0.5 * u))
    return x + f64(mlp_scale) * (mxq(act, 2, "e4m3") @ mxq(f64(wproj), 1, "e4m3").T)

@@ -1,0 +1,240 @@
+from contextlib import ExitStack
+
+import concourse.mybir as mybir
+from concourse.masks import make_identity
+
+F32 = mybir.dt.float32
+BF16 = mybir.dt.bfloat16
+U32 = mybir.dt.uint32
+U8 = mybir.dt.uint8
+FP8X4 = mybir.dt.float8_e4m3fn_x4
+ACT = mybir.ActivationFunctionType
+ALU = mybir.AluOpType
+
+P = 128
+PACK = 4
+K_PASS = P * PACK
+TOKENS = 4096
+D_MODEL = 1024
+D_FF = 512
+EPS = 1e-6
+PASSES_1 = D_MODEL // K_PASS
+TILES = 2
+GROUP = TILES * P
+GROUPS = TOKENS // GROUP
+HALF = 512
+PIECES = TILES * (D_MODEL // HALF)
+GPSIMD_PIECES = 2
+
+FLOPS = 2 * TOKENS * D_MODEL * D_FF * 2
+
+
+def tile_block_pc_t_kernel(tc, x_mid, wfc, wproj, mlp_scale, out):
+    nc = tc.nc
+    x_groups = x_mid.flatten_outer_dims().rearrange("(g p j) d -> g p j d", p=P, j=TILES)
+    out_groups = out.flatten_outer_dims().rearrange("(g p j) d -> g p j d", p=P, j=TILES)
+
+    with ExitStack() as stack:
+        keep = stack.enter_context(tc.tile_pool(name="keep", bufs=1))
+        psum_t = stack.enter_context(tc.psum_pool(name="psum_t", bufs=2))
+        psum_u = stack.enter_context(tc.psum_pool(name="psum_u", bufs=2))
+        psum_y = stack.enter_context(tc.psum_pool(name="psum_y", bufs=4))
+
+        ident = keep.tile([P, P], F32)
+        make_identity(nc, ident[:])
+        eps = keep.tile([P, 1], F32)
+        nc.vector.memset(eps[:], 12.0 * EPS)
+        gain = keep.tile([P, D_MODEL], BF16)
+        x_sb = [keep.tile([P, TILES, D_MODEL], BF16, name="x%d" % g) for g in range(GROUPS)]
+        w1_codes = keep.tile([P, PASSES_1, D_FF], U32, align_bytes=64)
+        w1_scales = keep.tile([P, PASSES_1, D_FF], U8, align_bytes=64)
+        w2_codes = keep.tile([P, D_MODEL], U32, align_bytes=64)
+        w2_scales = keep.tile([P, D_MODEL], U8, align_bytes=64)
+
+        def k_onto_partitions(rows_words, row_tiles, grouped_words, copy):
+            for c in range(PASSES_1):
+                for pair in range(row_tiles // 2):
+                    bank = psum_t.tile([P, 2, 2 * P], F32)
+                    for u in range(2):
+                        for jj in range(2):
+                            block = 2 * c + u
+                            nc.tensor.transpose(
+                                bank[:, u, jj * P : (jj + 1) * P],
+                                rows_words[:, 2 * pair + jj, block * P : (block + 1) * P],
+                                ident[:],
+                            )
+                    copy(
+                        out=grouped_words[:, c, pair * 2 * P : (pair + 1) * 2 * P, :],
+                        in_=bank[:].rearrange("p u r -> p r u"),
+                    )
+
+        with tc.tile_pool(name="prep", bufs=1) as prep:
+            w1_rows = prep.tile([P, PACK, D_MODEL], BF16)
+            nc.sync.dma_start(out=w1_rows[:], in_=wfc.rearrange("(p t) d -> p t d", t=PACK))
+            nc.sync.dma_start(out=x_sb[0][:], in_=x_groups[0])
+            nc.sync.dma_start(out=x_sb[1][:], in_=x_groups[1])
+            w2_rows = prep.tile([P, D_MODEL // P, D_FF], BF16)
+            nc.sync.dma_start(out=w2_rows[:], in_=wproj.rearrange("(i r) f -> r i f", r=P))
+            nc.sync.dma_start(out=x_sb[2][:], in_=x_groups[2])
+            nc.sync.dma_start(out=gain[:], in_=mlp_scale.partition_broadcast(P))
+            for g in range(3, GROUPS):
+                nc.sync.dma_start(out=x_sb[g][:], in_=x_groups[g])
+
+            w1_grouped = prep.tile([P, PASSES_1, D_FF, PACK], BF16, align_bytes=64)
+            k_onto_partitions(
+                w1_rows[:].rearrange("p t d -> p (t d)").bitcast(F32).rearrange("p (t w) -> p t w", t=PACK),
+                PACK,
+                w1_grouped[:]
+                .rearrange("p c r t -> p (c r t)")
+                .bitcast(F32)
+                .rearrange("p (c r u) -> p c r u", c=PASSES_1, u=2),
+                nc.vector.tensor_copy,
+            )
+            nc.vector.quantize_mx(
+                out=w1_codes[:].rearrange("p c r -> p (c r)").bitcast(FP8X4),
+                scales=w1_scales[:].rearrange("p c r -> p (c r)"),
+                in_=w1_grouped[:].rearrange("p c r t -> p (c r t)"),
+            )
+
+            w2_words = (
+                w2_rows[:]
+                .rearrange("p i f -> p (i f)")
+                .bitcast(F32)
+                .rearrange("p (i q u) -> p i q u", i=D_MODEL // P, u=2)
+            )
+            w2_grouped = prep.tile([P, D_MODEL, PACK], BF16, align_bytes=64)
+            w2_grouped_words = (
+                w2_grouped[:].rearrange("p r t -> p (r t)").bitcast(F32).rearrange("p (r u) -> p r u", u=2)
+            )
+            for pair in range(D_MODEL // (2 * P)):
+                bank = psum_t.tile([P, 2, 2 * P], F32)
+                for u in range(2):
+                    for ii in range(2):
+                        nc.tensor.transpose(
+                            bank[:, u, ii * P : (ii + 1) * P], w2_words[:, 2 * pair + ii, :, u], ident[:]
+                        )
+                nc.vector.tensor_copy(
+                    out=w2_grouped_words[:, pair * 2 * P : (pair + 1) * 2 * P, :],
+                    in_=bank[:].rearrange("p u r -> p r u"),
+                )
+            nc.vector.quantize_mx(
+                out=w2_codes[:].bitcast(FP8X4),
+                scales=w2_scales[:],
+                in_=w2_grouped[:].rearrange("p r t -> p (r t)"),
+            )
+
+        work = stack.enter_context(tc.tile_pool(name="work", bufs=3))
+        single = stack.enter_context(tc.tile_pool(name="single", bufs=1))
+        small = stack.enter_context(tc.tile_pool(name="small", bufs=4))
+        results = stack.enter_context(tc.tile_pool(name="results", bufs=3))
+
+        h_rows = {}
+        h_mx = {}
+        act_mx = {}
+
+        def normalise(g):
+            x = x_sb[g]
+            squares = single.tile([P, TILES, D_MODEL], BF16)
+            sum_sq = small.tile([P, TILES], F32)
+            for j in range(TILES):
+                nc.scalar.activation(
+                    out=squares[:, j, :], in_=x[:, j, :], func=ACT.Square, accum_out=sum_sq[:, j : j + 1]
+                )
+            norm = small.tile([P, TILES], F32)
+            nc.scalar.activation(
+                out=norm[:], in_=sum_sq[:], func=ACT.Sqrt, bias=eps[:, 0:1], scale=12.0 / D_MODEL
+            )
+            inv_norm = small.tile([P, TILES], F32)
+            nc.vector.reciprocal(out=inv_norm[:], in_=norm[:])
+            h = work.tile([P, TILES, D_MODEL], BF16)
+            for j in range(TILES):
+                nc.vector.tensor_scalar_mul(out=h[:, j, :], in0=x[:, j, :], scalar1=inv_norm[:, j : j + 1])
+            h_rows[g] = h
+
+        def quantise_h(g):
+            h = h_rows[g]
+            h_grouped = work.tile([P, PASSES_1, GROUP, PACK], BF16, align_bytes=64)
+            k_onto_partitions(
+                h[:].rearrange("p j d -> p (j d)").bitcast(F32).rearrange("p (j w) -> p j w", j=TILES),
+                TILES,
+                h_grouped[:]
+                .rearrange("p c r t -> p (c r t)")
+                .bitcast(F32)
+                .rearrange("p (c r u) -> p c r u", c=PASSES_1, u=2),
+                nc.scalar.copy,
+            )
+            h_codes = work.tile([P, PASSES_1, GROUP], U32, align_bytes=64)
+            h_scales = work.tile([P, PASSES_1, GROUP], U8, align_bytes=64)
+            nc.vector.quantize_mx(
+                out=h_codes[:].rearrange("p c r -> p (c r)").bitcast(FP8X4),
+                scales=h_scales[:].rearrange("p c r -> p (c r)"),
+                in_=h_grouped[:].rearrange("p c r t -> p (c r t)"),
+            )
+            h_mx[g] = (h_codes, h_scales)
+
+        def hidden_layer(g):
+            h_codes, h_scales = h_mx[g]
+            u_squared = work.tile([P, GROUP, PACK], BF16)
+            u_sign = work.tile([P, GROUP, PACK], BF16)
+            for j in range(TILES):
+                tokens = slice(j * P, (j + 1) * P)
+                u = psum_u.tile([P, PACK, P], F32)
+                for t in range(PACK):
+                    rows = slice(t * P, (t + 1) * P)
+                    for c in range(PASSES_1):
+                        nc.tensor.matmul_mx(
+                            out=u[:, t, :],
+                            lhsT=w1_codes[:, c, rows].bitcast(FP8X4),
+                            lhsT_scale=w1_scales[:, c, rows],
+                            rhs=h_codes[:, c, tokens].bitcast(FP8X4),
+                            rhs_scale=h_scales[:, c, tokens],
+                            start=(c == 0),
+                            stop=(c == PASSES_1 - 1),
+                        )
+                u_by_token = u[:].rearrange("p t r -> p r t")
+                nc.scalar.activation(out=u_squared[:, tokens, :], in_=u_by_token, func=ACT.Square)
+                nc.scalar.activation(out=u_sign[:, tokens, :], in_=u_by_token, func=ACT.Sign)
+            factor = work.tile([P, GROUP * PACK], BF16)
+            nc.vector.tensor_scalar_max(
+                out=factor[:], in0=u_sign[:].rearrange("p r t -> p (r t)"), scalar1=0.25
+            )
+            act = work.tile([P, GROUP * PACK], BF16, align_bytes=64)
+            nc.vector.tensor_tensor(
+                out=act[:], in0=u_squared[:].rearrange("p r t -> p (r t)"), in1=factor[:], op=ALU.mult
+            )
+            act_codes = work.tile([P, GROUP], U32, align_bytes=64)
+            act_scales = work.tile([P, GROUP], U8, align_bytes=64)
+            nc.vector.quantize_mx(out=act_codes[:].bitcast(FP8X4), scales=act_scales[:], in_=act[:])
+            act_mx[g] = (act_codes, act_scales)
+
+        def output_layer(g):
+            act_codes, act_scales = act_mx[g]
+            x = x_sb[g]
+            result = results.tile([P, TILES, D_MODEL], F32)
+            for j in range(TILES):
+                tokens = slice(j * P, (j + 1) * P)
+                for half in range(D_MODEL // HALF):
+                    cols = slice(half * HALF, (half + 1) * HALF)
+                    y = psum_y.tile([P, HALF], F32)
+                    nc.tensor.matmul_mx(
+                        out=y[:],
+                        lhsT=act_codes[:, tokens].bitcast(FP8X4),
+                        lhsT_scale=act_scales[:, tokens],
+                        rhs=w2_codes[:, cols].bitcast(FP8X4),
+                        rhs_scale=w2_scales[:, cols],
+                        start=True,
+                        stop=True,
+                    )
+                    nc.vector.tensor_tensor(out=result[:, j, cols], in0=y[:], in1=gain[:, cols], op=ALU.mult)
+                    piece = j * (D_MODEL // HALF) + half
+                    adder = nc.gpsimd if piece < GPSIMD_PIECES else nc.vector
+                    adder.tensor_tensor(
+                        out=result[:, j, cols], in0=result[:, j, cols], in1=x[:, j, cols], op=ALU.add
+                    )
+            nc.sync.dma_start(out=out_groups[g], in_=result[:])
+
+        stages = (normalise, quantise_h, hidden_layer, output_layer)
+        for step in range(GROUPS + len(stages) - 1):
+            for lag, stage in enumerate(stages):
+                if 0 <= step - lag < GROUPS:
+                    stage(step - lag)

@@ -19,222 +19,321 @@ D_MODEL = 1024
 D_FF = 512
 EPS = 1e-6
 PASSES_1 = D_MODEL // K_PASS
-TILES = 2
-GROUP = TILES * P
-GROUPS = TOKENS // GROUP
-HALF = 512
-PIECES = TILES * (D_MODEL // HALF)
-GPSIMD_PIECES = 2
+BANK = 512
+TURNED = 512
+TURNED_BLOCKS = TURNED // P
+
+GROUP_TILES = [1, 1] + [2] * 14 + [1, 1]
 
 FLOPS = 2 * TOKENS * D_MODEL * D_FF * 2
 
 
 def tile_block_pc_t_kernel(tc, x_mid, wfc, wproj, mlp_scale, out):
     nc = tc.nc
-    x_groups = x_mid.flatten_outer_dims().rearrange("(g p j) d -> g p j d", p=P, j=TILES)
-    out_groups = out.flatten_outer_dims().rearrange("(g p j) d -> g p j d", p=P, j=TILES)
+    x_flat = x_mid.flatten_outer_dims()
+    out_flat = out.flatten_outer_dims()
+    groups = len(GROUP_TILES)
+
+    def group_rows(flat, g):
+        n = GROUP_TILES[g]
+        first = sum(GROUP_TILES[:g]) * P
+        return flat[first : first + n * P, :].rearrange("(p j) d -> p j d", j=n)
 
     with ExitStack() as stack:
         keep = stack.enter_context(tc.tile_pool(name="keep", bufs=1))
-        psum_t = stack.enter_context(tc.psum_pool(name="psum_t", bufs=2))
+        psum_a = stack.enter_context(tc.psum_pool(name="psum_a", bufs=3))
+        psum_b = stack.enter_context(tc.psum_pool(name="psum_b", bufs=3))
         psum_u = stack.enter_context(tc.psum_pool(name="psum_u", bufs=2))
-        psum_y = stack.enter_context(tc.psum_pool(name="psum_y", bufs=4))
+        prep = stack.enter_context(tc.tile_pool(name="prep", bufs=1))
+        work = stack.enter_context(tc.tile_pool(name="work", bufs=3))
+        small = stack.enter_context(tc.tile_pool(name="small", bufs=4))
+        results = stack.enter_context(tc.tile_pool(name="results", bufs=3))
+        stack.enter_context(tc.manual_schedule())
 
         ident = keep.tile([P, P], F32)
-        make_identity(nc, ident[:])
         eps = keep.tile([P, 1], F32)
-        nc.vector.memset(eps[:], 12.0 * EPS)
         gain = keep.tile([P, D_MODEL], BF16)
-        x_sb = [keep.tile([P, TILES, D_MODEL], BF16, name="x%d" % g) for g in range(GROUPS)]
+        gain_f32 = keep.tile([P, TURNED], F32)
+        gain_column = keep.tile([P, TURNED_BLOCKS], F32)
+        x_sb = [keep.tile([P, GROUP_TILES[g], D_MODEL], BF16, name="x%d" % g) for g in range(groups)]
         w1_codes = keep.tile([P, PASSES_1, D_FF], U32, align_bytes=64)
         w1_scales = keep.tile([P, PASSES_1, D_FF], U8, align_bytes=64)
         w2_codes = keep.tile([P, D_MODEL], U32, align_bytes=64)
         w2_scales = keep.tile([P, D_MODEL], U8, align_bytes=64)
+        w1_rows = prep.tile([P, PACK, D_MODEL], BF16)
+        w2_rows = prep.tile([P, D_MODEL // P, D_FF], BF16)
+        w1_grouped = prep.tile([P, PASSES_1, D_FF, PACK], BF16, align_bytes=64)
+        w2_grouped = prep.tile([P, D_MODEL, PACK], BF16, align_bytes=64)
+        squares = prep.tile([P, D_MODEL], BF16)
 
-        def k_onto_partitions(rows_words, row_tiles, grouped_words, copy):
+        nc.vector.memset(eps[:], 12.0 * EPS)
+        make_identity(nc, ident[:])
+        nc.sync.dma_start(out=x_sb[0][:], in_=group_rows(x_flat, 0))
+        nc.sync.dma_start(out=w1_rows[:], in_=wfc.rearrange("(p t) d -> p t d", t=PACK))
+        nc.sync.dma_start(out=x_sb[1][:], in_=group_rows(x_flat, 1))
+        nc.sync.dma_start(out=x_sb[2][:], in_=group_rows(x_flat, 2))
+        nc.sync.dma_start(out=w2_rows[:], in_=wproj.rearrange("(i r) f -> r i f", r=P))
+        nc.sync.dma_start(out=gain[:], in_=mlp_scale.partition_broadcast(P))
+        for g in range(3, groups):
+            nc.sync.dma_start(out=x_sb[g][:], in_=group_rows(x_flat, g))
+
+        sum_sq, h_rows, h_bank, h_grouped, h_mx, u_bank = {}, {}, {}, {}, {}, {}
+        factor, u_squared, act_mx, y_bank, yt_bank, z_sb, zt_bank, result = {}, {}, {}, {}, {}, {}, {}, {}
+
+        def words(ap, pattern, **sizes):
+            return ap.rearrange(pattern, **sizes).bitcast(F32)
+
+        def prepare_w1():
+            w1_words = words(w1_rows[:], "p t d -> p (t d)").rearrange("p (t w) -> p t w", t=PACK)
+            w1_out = words(w1_grouped[:], "p c r t -> p (c r t)").rearrange(
+                "p (c r u) -> p c r u", c=PASSES_1, u=2
+            )
             for c in range(PASSES_1):
-                for pair in range(row_tiles // 2):
-                    bank = psum_t.tile([P, 2, 2 * P], F32)
+                for pair in range(2):
+                    bank = psum_b.tile([P, 2, 2 * P], F32)
                     for u in range(2):
                         for jj in range(2):
                             block = 2 * c + u
                             nc.tensor.transpose(
                                 bank[:, u, jj * P : (jj + 1) * P],
-                                rows_words[:, 2 * pair + jj, block * P : (block + 1) * P],
+                                w1_words[:, 2 * pair + jj, block * P : (block + 1) * P],
                                 ident[:],
                             )
+                    copy = nc.vector.tensor_copy if pair == 0 else nc.scalar.copy
                     copy(
-                        out=grouped_words[:, c, pair * 2 * P : (pair + 1) * 2 * P, :],
+                        out=w1_out[:, c, pair * 2 * P : (pair + 1) * 2 * P, :],
                         in_=bank[:].rearrange("p u r -> p r u"),
                     )
+                nc.vector.quantize_mx(
+                    out=w1_codes[:, c, :].bitcast(FP8X4),
+                    scales=w1_scales[:, c, :],
+                    in_=w1_grouped[:, c, :, :].rearrange("p r t -> p (r t)"),
+                )
 
-        with tc.tile_pool(name="prep", bufs=1) as prep:
-            w1_rows = prep.tile([P, PACK, D_MODEL], BF16)
-            nc.sync.dma_start(out=w1_rows[:], in_=wfc.rearrange("(p t) d -> p t d", t=PACK))
-            nc.sync.dma_start(out=x_sb[0][:], in_=x_groups[0])
-            nc.sync.dma_start(out=x_sb[1][:], in_=x_groups[1])
-            w2_rows = prep.tile([P, D_MODEL // P, D_FF], BF16)
-            nc.sync.dma_start(out=w2_rows[:], in_=wproj.rearrange("(i r) f -> r i f", r=P))
-            nc.sync.dma_start(out=x_sb[2][:], in_=x_groups[2])
-            nc.sync.dma_start(out=gain[:], in_=mlp_scale.partition_broadcast(P))
-            for g in range(3, GROUPS):
-                nc.sync.dma_start(out=x_sb[g][:], in_=x_groups[g])
-
-            w1_grouped = prep.tile([P, PASSES_1, D_FF, PACK], BF16, align_bytes=64)
-            k_onto_partitions(
-                w1_rows[:].rearrange("p t d -> p (t d)").bitcast(F32).rearrange("p (t w) -> p t w", t=PACK),
-                PACK,
-                w1_grouped[:]
-                .rearrange("p c r t -> p (c r t)")
-                .bitcast(F32)
-                .rearrange("p (c r u) -> p c r u", c=PASSES_1, u=2),
-                nc.vector.tensor_copy,
+        def prepare_w2():
+            w2_words = words(w2_rows[:], "p i f -> p (i f)").rearrange(
+                "p (i q u) -> p i q u", i=D_MODEL // P, u=2
             )
-            nc.vector.quantize_mx(
-                out=w1_codes[:].rearrange("p c r -> p (c r)").bitcast(FP8X4),
-                scales=w1_scales[:].rearrange("p c r -> p (c r)"),
-                in_=w1_grouped[:].rearrange("p c r t -> p (c r t)"),
-            )
-
-            w2_words = (
-                w2_rows[:]
-                .rearrange("p i f -> p (i f)")
-                .bitcast(F32)
-                .rearrange("p (i q u) -> p i q u", i=D_MODEL // P, u=2)
-            )
-            w2_grouped = prep.tile([P, D_MODEL, PACK], BF16, align_bytes=64)
-            w2_grouped_words = (
-                w2_grouped[:].rearrange("p r t -> p (r t)").bitcast(F32).rearrange("p (r u) -> p r u", u=2)
-            )
+            w2_out = words(w2_grouped[:], "p r t -> p (r t)").rearrange("p (r u) -> p r u", u=2)
             for pair in range(D_MODEL // (2 * P)):
-                bank = psum_t.tile([P, 2, 2 * P], F32)
+                bank = psum_b.tile([P, 2, 2 * P], F32)
                 for u in range(2):
                     for ii in range(2):
                         nc.tensor.transpose(
                             bank[:, u, ii * P : (ii + 1) * P], w2_words[:, 2 * pair + ii, :, u], ident[:]
                         )
                 nc.vector.tensor_copy(
-                    out=w2_grouped_words[:, pair * 2 * P : (pair + 1) * 2 * P, :],
+                    out=w2_out[:, pair * 2 * P : (pair + 1) * 2 * P, :],
                     in_=bank[:].rearrange("p u r -> p r u"),
                 )
-            nc.vector.quantize_mx(
-                out=w2_codes[:].bitcast(FP8X4),
-                scales=w2_scales[:],
-                in_=w2_grouped[:].rearrange("p r t -> p (r t)"),
-            )
-
-        work = stack.enter_context(tc.tile_pool(name="work", bufs=3))
-        single = stack.enter_context(tc.tile_pool(name="single", bufs=1))
-        small = stack.enter_context(tc.tile_pool(name="small", bufs=4))
-        results = stack.enter_context(tc.tile_pool(name="results", bufs=3))
-
-        h_rows = {}
-        h_mx = {}
-        act_mx = {}
-
-        def normalise(g):
-            x = x_sb[g]
-            squares = single.tile([P, TILES, D_MODEL], BF16)
-            sum_sq = small.tile([P, TILES], F32)
-            for j in range(TILES):
-                nc.scalar.activation(
-                    out=squares[:, j, :], in_=x[:, j, :], func=ACT.Square, accum_out=sum_sq[:, j : j + 1]
+            for half in range(2):
+                cols = slice(half * D_MODEL // 2, (half + 1) * D_MODEL // 2)
+                nc.vector.quantize_mx(
+                    out=w2_codes[:, cols].bitcast(FP8X4),
+                    scales=w2_scales[:, cols],
+                    in_=w2_grouped[:, cols, :].rearrange("p r t -> p (r t)"),
                 )
-            norm = small.tile([P, TILES], F32)
-            nc.scalar.activation(
-                out=norm[:], in_=sum_sq[:], func=ACT.Sqrt, bias=eps[:, 0:1], scale=12.0 / D_MODEL
-            )
-            inv_norm = small.tile([P, TILES], F32)
-            nc.vector.reciprocal(out=inv_norm[:], in_=norm[:])
-            h = work.tile([P, TILES, D_MODEL], BF16)
-            for j in range(TILES):
-                nc.vector.tensor_scalar_mul(out=h[:, j, :], in0=x[:, j, :], scalar1=inv_norm[:, j : j + 1])
+
+        def prepare_gain_column():
+            nc.vector.tensor_copy(out=gain_f32[:], in_=gain[:, 0:TURNED])
+            bank = psum_b.tile([P, TURNED_BLOCKS, P], F32)
+            for b in range(TURNED_BLOCKS):
+                nc.tensor.transpose(bank[:, b, :], gain_f32[:, b * P : (b + 1) * P], ident[:])
+            nc.vector.tensor_copy(out=gain_column[:], in_=bank[:, :, 0])
+
+
+        def scalar_sum_of_squares(g):
+            n = GROUP_TILES[g]
+            sums = small.tile([P, n], F32)
+            for j in range(n):
+                nc.scalar.activation(
+                    out=squares[:], in_=x_sb[g][:, j, :], func=ACT.Square, accum_out=sums[:, j : j + 1]
+                )
+            norm = small.tile([P, n], F32)
+            nc.scalar.activation(out=norm[:], in_=sums[:], func=ACT.Sqrt, bias=eps[:, 0:1], scale=12.0 / D_MODEL)
+            sum_sq[g] = norm
+
+        def vector_normalise(g):
+            n = GROUP_TILES[g]
+            inv_norm = small.tile([P, n], F32)
+            nc.vector.reciprocal(out=inv_norm[:], in_=sum_sq[g][:])
+            h = work.tile([P, n, D_MODEL], BF16)
+            for j in range(n):
+                nc.vector.tensor_scalar_mul(out=h[:, j, :], in0=x_sb[g][:, j, :], scalar1=inv_norm[:, j : j + 1])
             h_rows[g] = h
 
-        def quantise_h(g):
-            h = h_rows[g]
-            h_grouped = work.tile([P, PASSES_1, GROUP, PACK], BF16, align_bytes=64)
-            k_onto_partitions(
-                h[:].rearrange("p j d -> p (j d)").bitcast(F32).rearrange("p (j w) -> p j w", j=TILES),
-                TILES,
-                h_grouped[:]
-                .rearrange("p c r t -> p (c r t)")
-                .bitcast(F32)
-                .rearrange("p (c r u) -> p c r u", c=PASSES_1, u=2),
-                nc.scalar.copy,
+        def tensor_turn_h(g):
+            n = GROUP_TILES[g]
+            h_words = words(h_rows[g][:], "p j d -> p (j d)").rearrange("p (j w) -> p j w", j=n)
+            for j in range(n):
+                bank = psum_b.tile([P, PASSES_1, 2, P], F32)
+                for c in range(PASSES_1):
+                    for u in range(2):
+                        block = 2 * c + u
+                        nc.tensor.transpose(bank[:, c, u, :], h_words[:, j, block * P : (block + 1) * P], ident[:])
+                h_bank[g, j] = bank
+
+        def scalar_group_h(g):
+            n = GROUP_TILES[g]
+            grouped = work.tile([P, n, PASSES_1, P, PACK], BF16, align_bytes=64)
+            grouped_words = words(grouped[:], "p j c r t -> p (j c r t)").rearrange(
+                "p (j c r u) -> p j c r u", j=n, c=PASSES_1, u=2
             )
-            h_codes = work.tile([P, PASSES_1, GROUP], U32, align_bytes=64)
-            h_scales = work.tile([P, PASSES_1, GROUP], U8, align_bytes=64)
+            for j in range(n):
+                nc.scalar.copy(out=grouped_words[:, j], in_=h_bank[g, j][:].rearrange("p c u r -> p c r u"))
+            h_grouped[g] = grouped
+
+        def vector_quantise_h(g):
+            n = GROUP_TILES[g]
+            h_codes = work.tile([P, n, PASSES_1, P], U32, align_bytes=64)
+            h_scales = work.tile([P, n, PASSES_1, P], U8, align_bytes=64)
             nc.vector.quantize_mx(
-                out=h_codes[:].rearrange("p c r -> p (c r)").bitcast(FP8X4),
-                scales=h_scales[:].rearrange("p c r -> p (c r)"),
-                in_=h_grouped[:].rearrange("p c r t -> p (c r t)"),
+                out=h_codes[:].rearrange("p j c r -> p (j c r)").bitcast(FP8X4),
+                scales=h_scales[:].rearrange("p j c r -> p (j c r)"),
+                in_=h_grouped[g][:].rearrange("p j c r t -> p (j c r t)"),
             )
             h_mx[g] = (h_codes, h_scales)
 
-        def hidden_layer(g):
-            h_codes, h_scales = h_mx[g]
-            u_squared = work.tile([P, GROUP, PACK], BF16)
-            u_sign = work.tile([P, GROUP, PACK], BF16)
-            for j in range(TILES):
-                tokens = slice(j * P, (j + 1) * P)
-                u = psum_u.tile([P, PACK, P], F32)
+        def tensor_hidden(g):
+            codes, scales = h_mx[g]
+            for j in range(GROUP_TILES[g]):
+                bank = psum_u.tile([P, PACK, P], F32)
                 for t in range(PACK):
                     rows = slice(t * P, (t + 1) * P)
                     for c in range(PASSES_1):
                         nc.tensor.matmul_mx(
-                            out=u[:, t, :],
+                            out=bank[:, t, :],
                             lhsT=w1_codes[:, c, rows].bitcast(FP8X4),
                             lhsT_scale=w1_scales[:, c, rows],
-                            rhs=h_codes[:, c, tokens].bitcast(FP8X4),
-                            rhs_scale=h_scales[:, c, tokens],
+                            rhs=codes[:, j, c, :].bitcast(FP8X4),
+                            rhs_scale=scales[:, j, c, :],
                             start=(c == 0),
                             stop=(c == PASSES_1 - 1),
                         )
-                u_by_token = u[:].rearrange("p t r -> p r t")
-                nc.scalar.activation(out=u_squared[:, tokens, :], in_=u_by_token, func=ACT.Square)
-                nc.scalar.activation(out=u_sign[:, tokens, :], in_=u_by_token, func=ACT.Sign)
-            factor = work.tile([P, GROUP * PACK], BF16)
-            nc.vector.tensor_scalar_max(
-                out=factor[:], in0=u_sign[:].rearrange("p r t -> p (r t)"), scalar1=0.25
-            )
-            act = work.tile([P, GROUP * PACK], BF16, align_bytes=64)
+                u_bank[g, j] = bank
+
+        def activate(g):
+            n = GROUP_TILES[g]
+            sq = work.tile([P, n, P, PACK], BF16)
+            fac = work.tile([P, n, P, PACK], BF16)
+            for j in range(n):
+                k = n - 1 - j
+                nc.scalar.activation(
+                    out=sq[:, j, :, :], in_=u_bank[g, j][:].rearrange("p t r -> p r t"), func=ACT.Square
+                )
+                nc.vector.tensor_scalar(
+                    out=fac[:, k, :, :],
+                    in0=u_bank[g, k][:].rearrange("p t r -> p r t"),
+                    scalar1=0.0,
+                    scalar2=0.25,
+                    op0=ALU.is_ge,
+                    op1=ALU.max,
+                )
+            u_squared[g], factor[g] = sq, fac
+
+        def vector_quantise_act(g):
+            n = GROUP_TILES[g]
+            act = work.tile([P, n * P * PACK], BF16, align_bytes=64)
             nc.vector.tensor_tensor(
-                out=act[:], in0=u_squared[:].rearrange("p r t -> p (r t)"), in1=factor[:], op=ALU.mult
+                out=act[:],
+                in0=u_squared[g][:].rearrange("p j r t -> p (j r t)"),
+                in1=factor[g][:].rearrange("p j r t -> p (j r t)"),
+                op=ALU.mult,
             )
-            act_codes = work.tile([P, GROUP], U32, align_bytes=64)
-            act_scales = work.tile([P, GROUP], U8, align_bytes=64)
+            act_codes = work.tile([P, n * P], U32, align_bytes=64)
+            act_scales = work.tile([P, n * P], U8, align_bytes=64)
             nc.vector.quantize_mx(out=act_codes[:].bitcast(FP8X4), scales=act_scales[:], in_=act[:])
             act_mx[g] = (act_codes, act_scales)
 
-        def output_layer(g):
-            act_codes, act_scales = act_mx[g]
-            x = x_sb[g]
-            result = results.tile([P, TILES, D_MODEL], F32)
-            for j in range(TILES):
-                tokens = slice(j * P, (j + 1) * P)
-                for half in range(D_MODEL // HALF):
-                    cols = slice(half * HALF, (half + 1) * HALF)
-                    y = psum_y.tile([P, HALF], F32)
+        def tensor_output(g):
+            codes, scales = act_mx[g]
+            n = GROUP_TILES[g]
+            per_bank = BANK // (n * P)
+            for first in range(0, TURNED_BLOCKS, per_bank):
+                bank = psum_b.tile([P, per_bank, n * P], F32)
+                for b in range(first, first + per_bank):
+                    channels = slice(b * P, (b + 1) * P)
                     nc.tensor.matmul_mx(
-                        out=y[:],
-                        lhsT=act_codes[:, tokens].bitcast(FP8X4),
-                        lhsT_scale=act_scales[:, tokens],
-                        rhs=w2_codes[:, cols].bitcast(FP8X4),
-                        rhs_scale=w2_scales[:, cols],
+                        out=bank[:, b - first, :],
+                        lhsT=w2_codes[:, channels].bitcast(FP8X4),
+                        lhsT_scale=w2_scales[:, channels],
+                        rhs=codes[:].bitcast(FP8X4),
+                        rhs_scale=scales[:],
                         start=True,
                         stop=True,
                     )
-                    nc.vector.tensor_tensor(out=result[:, j, cols], in0=y[:], in1=gain[:, cols], op=ALU.mult)
-                    piece = j * (D_MODEL // HALF) + half
-                    adder = nc.gpsimd if piece < GPSIMD_PIECES else nc.vector
-                    adder.tensor_tensor(
-                        out=result[:, j, cols], in0=result[:, j, cols], in1=x[:, j, cols], op=ALU.add
-                    )
-            nc.sync.dma_start(out=out_groups[g], in_=result[:])
+                    yt_bank[g, b] = bank[:, b - first, :]
+            for j in range(n):
+                tokens = slice(j * P, (j + 1) * P)
+                bank = psum_a.tile([P, BANK], F32)
+                nc.tensor.matmul_mx(
+                    out=bank[:],
+                    lhsT=codes[:, tokens].bitcast(FP8X4),
+                    lhsT_scale=scales[:, tokens],
+                    rhs=w2_codes[:, TURNED:D_MODEL].bitcast(FP8X4),
+                    rhs_scale=w2_scales[:, TURNED:D_MODEL],
+                    start=True,
+                    stop=True,
+                )
+                y_bank[g, j] = bank
 
-        stages = (normalise, quantise_h, hidden_layer, output_layer)
-        for step in range(GROUPS + len(stages) - 1):
-            for lag, stage in enumerate(stages):
-                if 0 <= step - lag < GROUPS:
-                    stage(step - lag)
+        def scalar_gain(g):
+            n = GROUP_TILES[g]
+            z = work.tile([P, TURNED_BLOCKS, n * P], F32)
+            for b in range(TURNED_BLOCKS):
+                nc.scalar.activation(
+                    out=z[:, b, :], in_=yt_bank[g, b], func=ACT.Copy, scale=gain_column[:, b : b + 1]
+                )
+            z_sb[g] = z
+
+        def vector_gain(g):
+            n = GROUP_TILES[g]
+            res = results.tile([P, n, D_MODEL], F32)
+            for j in range(n):
+                cols = slice(TURNED, D_MODEL)
+                nc.vector.tensor_tensor(out=res[:, j, cols], in0=y_bank[g, j][:], in1=gain[:, cols], op=ALU.mult)
+                nc.gpsimd.tensor_tensor(
+                    out=res[:, j, cols], in0=res[:, j, cols], in1=x_sb[g][:, j, cols], op=ALU.add
+                )
+            result[g] = res
+
+        def tensor_turn_z(g):
+            for j in range(GROUP_TILES[g]):
+                bank = psum_a.tile([P, TURNED_BLOCKS, P], F32)
+                for b in range(TURNED_BLOCKS):
+                    nc.tensor.transpose(bank[:, b, :], z_sb[g][:, b, j * P : (j + 1) * P], ident[:])
+                zt_bank[g, j] = bank
+
+        def vector_finish(g):
+            for j in range(GROUP_TILES[g]):
+                nc.vector.tensor_tensor(
+                    out=result[g][:, j, 0:TURNED],
+                    in0=zt_bank[g, j][:].rearrange("p b r -> p (b r)"),
+                    in1=x_sb[g][:, j, 0:TURNED],
+                    op=ALU.add,
+                )
+            nc.sync.dma_start(out=group_rows(out_flat, g), in_=result[g][:])
+
+        def at(stage, g):
+            if 0 <= g < groups:
+                stage(g)
+
+        for step in range(groups + 4):
+            if step == 2:
+                prepare_w1()
+            if step == 3:
+                prepare_w2()
+                prepare_gain_column()
+            at(tensor_hidden, step - 3)
+            at(scalar_gain, step - 4)
+            at(vector_gain, step - 4)
+            at(activate, step - 3)
+            at(tensor_turn_h, step - 2)
+            at(tensor_turn_z, step - 4)
+            at(scalar_group_h, step - 2)
+            at(vector_finish, step - 4)
+            at(vector_quantise_act, step - 3)
+            at(tensor_output, step - 3)
+            at(vector_normalise, step - 1)
+            at(scalar_sum_of_squares, step)
+            at(vector_quantise_h, step - 2)

@@ -23,7 +23,7 @@ BANK = 512
 TURNED = 512
 TURNED_BLOCKS = TURNED // P
 
-GROUP_TILES = [1, 1] + [2] * 14 + [1, 1]
+GROUP_TILES = [1] * 32
 
 FLOPS = 2 * TOKENS * D_MODEL * D_FF * 2
 
@@ -45,9 +45,9 @@ def tile_block_pc_t_kernel(tc, x_mid, wfc, wproj, mlp_scale, out):
         psum_b = stack.enter_context(tc.psum_pool(name="psum_b", bufs=3))
         psum_u = stack.enter_context(tc.psum_pool(name="psum_u", bufs=2))
         prep = stack.enter_context(tc.tile_pool(name="prep", bufs=1))
-        work = stack.enter_context(tc.tile_pool(name="work", bufs=3))
-        small = stack.enter_context(tc.tile_pool(name="small", bufs=4))
-        results = stack.enter_context(tc.tile_pool(name="results", bufs=3))
+        work = stack.enter_context(tc.tile_pool(name="work", bufs=4))
+        small = stack.enter_context(tc.tile_pool(name="small", bufs=6))
+        results = stack.enter_context(tc.tile_pool(name="results", bufs=5))
         stack.enter_context(tc.manual_schedule())
 
         ident = keep.tile([P, P], F32)
@@ -78,61 +78,58 @@ def tile_block_pc_t_kernel(tc, x_mid, wfc, wproj, mlp_scale, out):
             nc.sync.dma_start(out=x_sb[g][:], in_=group_rows(x_flat, g))
 
         sum_sq, h_rows, h_bank, h_grouped, h_mx, u_bank = {}, {}, {}, {}, {}, {}
-        factor, u_squared, act_mx, y_bank, yt_bank, z_sb, zt_bank, result = {}, {}, {}, {}, {}, {}, {}, {}
+        factor, u_squared, act_rows, act_mx, y_bank, yt_bank, z_sb, zt_bank = {}, {}, {}, {}, {}, {}, {}, {}
+        result = {}
 
         def words(ap, pattern, **sizes):
             return ap.rearrange(pattern, **sizes).bitcast(F32)
 
-        def prepare_w1():
+        def prepare_w1(c):
             w1_words = words(w1_rows[:], "p t d -> p (t d)").rearrange("p (t w) -> p t w", t=PACK)
             w1_out = words(w1_grouped[:], "p c r t -> p (c r t)").rearrange(
                 "p (c r u) -> p c r u", c=PASSES_1, u=2
             )
-            for c in range(PASSES_1):
-                for pair in range(2):
-                    bank = psum_b.tile([P, 2, 2 * P], F32)
-                    for u in range(2):
-                        for jj in range(2):
-                            block = 2 * c + u
-                            nc.tensor.transpose(
-                                bank[:, u, jj * P : (jj + 1) * P],
-                                w1_words[:, 2 * pair + jj, block * P : (block + 1) * P],
-                                ident[:],
-                            )
-                    copy = nc.vector.tensor_copy if pair == 0 else nc.scalar.copy
-                    copy(
-                        out=w1_out[:, c, pair * 2 * P : (pair + 1) * 2 * P, :],
-                        in_=bank[:].rearrange("p u r -> p r u"),
-                    )
-                nc.vector.quantize_mx(
-                    out=w1_codes[:, c, :].bitcast(FP8X4),
-                    scales=w1_scales[:, c, :],
-                    in_=w1_grouped[:, c, :, :].rearrange("p r t -> p (r t)"),
+            for pair in range(2):
+                bank = psum_b.tile([P, 2, 2 * P], F32)
+                for u in range(2):
+                    for jj in range(2):
+                        block = 2 * c + u
+                        nc.tensor.transpose(
+                            bank[:, u, jj * P : (jj + 1) * P],
+                            w1_words[:, 2 * pair + jj, block * P : (block + 1) * P],
+                            ident[:],
+                        )
+                nc.vector.tensor_copy(
+                    out=w1_out[:, c, pair * 2 * P : (pair + 1) * 2 * P, :],
+                    in_=bank[:].rearrange("p u r -> p r u"),
                 )
+            nc.vector.quantize_mx(
+                out=w1_codes[:, c, :].bitcast(FP8X4),
+                scales=w1_scales[:, c, :],
+                in_=w1_grouped[:, c, :, :].rearrange("p r t -> p (r t)"),
+            )
 
-        def prepare_w2():
+        def prepare_w2(pair):
             w2_words = words(w2_rows[:], "p i f -> p (i f)").rearrange(
                 "p (i q u) -> p i q u", i=D_MODEL // P, u=2
             )
             w2_out = words(w2_grouped[:], "p r t -> p (r t)").rearrange("p (r u) -> p r u", u=2)
-            for pair in range(D_MODEL // (2 * P)):
-                bank = psum_b.tile([P, 2, 2 * P], F32)
-                for u in range(2):
-                    for ii in range(2):
-                        nc.tensor.transpose(
-                            bank[:, u, ii * P : (ii + 1) * P], w2_words[:, 2 * pair + ii, :, u], ident[:]
-                        )
-                nc.vector.tensor_copy(
-                    out=w2_out[:, pair * 2 * P : (pair + 1) * 2 * P, :],
-                    in_=bank[:].rearrange("p u r -> p r u"),
-                )
-            for half in range(2):
-                cols = slice(half * D_MODEL // 2, (half + 1) * D_MODEL // 2)
-                nc.vector.quantize_mx(
-                    out=w2_codes[:, cols].bitcast(FP8X4),
-                    scales=w2_scales[:, cols],
-                    in_=w2_grouped[:, cols, :].rearrange("p r t -> p (r t)"),
-                )
+            cols = slice(pair * 2 * P, (pair + 1) * 2 * P)
+            bank = psum_b.tile([P, 2, 2 * P], F32)
+            for u in range(2):
+                for ii in range(2):
+                    nc.tensor.transpose(
+                        bank[:, u, ii * P : (ii + 1) * P], w2_words[:, 2 * pair + ii, :, u], ident[:]
+                    )
+            nc.vector.tensor_copy(out=w2_out[:, cols, :], in_=bank[:].rearrange("p u r -> p r u"))
+
+        def quantise_w2(half):
+            cols = slice(half * D_MODEL // 2, (half + 1) * D_MODEL // 2)
+            nc.vector.quantize_mx(
+                out=w2_codes[:, cols].bitcast(FP8X4),
+                scales=w2_scales[:, cols],
+                in_=w2_grouped[:, cols, :].rearrange("p r t -> p (r t)"),
+            )
 
         def prepare_gain_column():
             nc.vector.tensor_copy(out=gain_f32[:], in_=gain[:, 0:TURNED])
@@ -231,7 +228,7 @@ def tile_block_pc_t_kernel(tc, x_mid, wfc, wproj, mlp_scale, out):
                 )
             u_squared[g], factor[g] = sq, fac
 
-        def vector_quantise_act(g):
+        def vector_multiply(g):
             n = GROUP_TILES[g]
             act = work.tile([P, n * P * PACK], BF16, align_bytes=64)
             nc.vector.tensor_tensor(
@@ -240,9 +237,13 @@ def tile_block_pc_t_kernel(tc, x_mid, wfc, wproj, mlp_scale, out):
                 in1=factor[g][:].rearrange("p j r t -> p (j r t)"),
                 op=ALU.mult,
             )
+            act_rows[g] = act
+
+        def vector_quantise_act(g):
+            n = GROUP_TILES[g]
             act_codes = work.tile([P, n * P], U32, align_bytes=64)
             act_scales = work.tile([P, n * P], U8, align_bytes=64)
-            nc.vector.quantize_mx(out=act_codes[:].bitcast(FP8X4), scales=act_scales[:], in_=act[:])
+            nc.vector.quantize_mx(out=act_codes[:].bitcast(FP8X4), scales=act_scales[:], in_=act_rows[g][:])
             act_mx[g] = (act_codes, act_scales)
 
         def tensor_output(g):
@@ -318,22 +319,33 @@ def tile_block_pc_t_kernel(tc, x_mid, wfc, wproj, mlp_scale, out):
             if 0 <= g < groups:
                 stage(g)
 
-        for step in range(groups + 4):
+        at(scalar_sum_of_squares, 0)
+        at(scalar_sum_of_squares, 1)
+        for step in range(groups + 7):
             if step == 2:
-                prepare_w1()
+                prepare_w1(0)
             if step == 3:
-                prepare_w2()
+                prepare_w1(1)
+                prepare_w2(0)
+                prepare_w2(1)
+            if step == 4:
+                quantise_w2(0)
+                prepare_w2(2)
+                prepare_w2(3)
+            if step == 5:
+                quantise_w2(1)
                 prepare_gain_column()
-            at(tensor_hidden, step - 3)
-            at(scalar_gain, step - 4)
-            at(vector_gain, step - 4)
-            at(activate, step - 3)
+            at(vector_gain, step - 7)
+            at(tensor_output, step - 6)
+            at(vector_finish, step - 7)
             at(tensor_turn_h, step - 2)
-            at(tensor_turn_z, step - 4)
+            at(activate, step - 5)
+            at(scalar_gain, step - 6)
+            at(tensor_hidden, step - 4)
             at(scalar_group_h, step - 2)
-            at(vector_finish, step - 4)
-            at(vector_quantise_act, step - 3)
-            at(tensor_output, step - 3)
+            at(vector_quantise_h, step - 3)
+            at(tensor_turn_z, step - 6)
+            at(scalar_sum_of_squares, step + 2)
+            at(vector_multiply, step - 5)
             at(vector_normalise, step - 1)
-            at(scalar_sum_of_squares, step)
-            at(vector_quantise_h, step - 2)
+            at(vector_quantise_act, step - 5)

@@ -23,7 +23,7 @@ BANK = 512
 TURNED = 512
 TURNED_BLOCKS = TURNED // P
 
-GROUP_TILES = [1] * 32
+GROUP_TILES = [1, 1] + [2] * 14 + [1, 1]
 
 FLOPS = 2 * TOKENS * D_MODEL * D_FF * 2
 
@@ -41,19 +41,21 @@ def tile_block_pc_t_kernel(tc, x_mid, wfc, wproj, mlp_scale, out):
 
     with ExitStack() as stack:
         keep = stack.enter_context(tc.tile_pool(name="keep", bufs=1))
-        psum_a = stack.enter_context(tc.psum_pool(name="psum_a", bufs=3))
-        psum_b = stack.enter_context(tc.psum_pool(name="psum_b", bufs=3))
+        psum_y = stack.enter_context(tc.psum_pool(name="psum_y", bufs=2))
+        psum_t = stack.enter_context(tc.psum_pool(name="psum_t", bufs=4))
         psum_u = stack.enter_context(tc.psum_pool(name="psum_u", bufs=2))
         prep = stack.enter_context(tc.tile_pool(name="prep", bufs=1))
-        work = stack.enter_context(tc.tile_pool(name="work", bufs=4))
-        small = stack.enter_context(tc.tile_pool(name="small", bufs=6))
-        results = stack.enter_context(tc.tile_pool(name="results", bufs=5))
+        work = stack.enter_context(tc.tile_pool(name="work", bufs=3))
+        small = stack.enter_context(tc.tile_pool(name="small", bufs=8))
+        results = stack.enter_context(tc.tile_pool(name="results", bufs=4))
         stack.enter_context(tc.manual_schedule())
 
         ident = keep.tile([P, P], F32)
         eps = keep.tile([P, 1], F32)
-        gain = keep.tile([P, D_MODEL], BF16)
-        gain_f32 = keep.tile([P, TURNED], F32)
+        gain = keep.tile([P, D_MODEL - TURNED], BF16)
+        gain_blocks = keep.tile([P, P], BF16)
+        gain_rows = keep.tile([P, P], F32)
+        zeros = keep.tile([P, BANK], BF16)
         gain_column = keep.tile([P, TURNED_BLOCKS], F32)
         x_sb = [keep.tile([P, GROUP_TILES[g], D_MODEL], BF16, name="x%d" % g) for g in range(groups)]
         w1_codes = keep.tile([P, PASSES_1, D_FF], U32, align_bytes=64)
@@ -66,31 +68,35 @@ def tile_block_pc_t_kernel(tc, x_mid, wfc, wproj, mlp_scale, out):
         w2_grouped = prep.tile([P, D_MODEL, PACK], BF16, align_bytes=64)
         squares = prep.tile([P, D_MODEL], BF16)
 
+        nc.vector.memset(zeros[:], 0.0)
         nc.vector.memset(eps[:], 12.0 * EPS)
+        nc.vector.memset(gain_blocks[:], 0.0)
         make_identity(nc, ident[:])
         nc.sync.dma_start(out=x_sb[0][:], in_=group_rows(x_flat, 0))
-        nc.sync.dma_start(out=w1_rows[:], in_=wfc.rearrange("(p t) d -> p t d", t=PACK))
         nc.sync.dma_start(out=x_sb[1][:], in_=group_rows(x_flat, 1))
+        nc.sync.dma_start(out=w1_rows[:], in_=wfc.rearrange("(p t) d -> p t d", t=PACK))
         nc.sync.dma_start(out=x_sb[2][:], in_=group_rows(x_flat, 2))
         nc.sync.dma_start(out=w2_rows[:], in_=wproj.rearrange("(i r) f -> r i f", r=P))
-        nc.sync.dma_start(out=gain[:], in_=mlp_scale.partition_broadcast(P))
-        for g in range(3, groups):
+        nc.sync.dma_start(
+            out=gain_blocks[0:TURNED_BLOCKS, :], in_=mlp_scale[0:TURNED].rearrange("(b c) -> b c", c=P)
+        )
+        nc.sync.dma_start(out=x_sb[3][:], in_=group_rows(x_flat, 3))
+        nc.sync.dma_start(out=gain[:], in_=mlp_scale[TURNED:D_MODEL].partition_broadcast(P))
+        for g in range(4, groups):
             nc.sync.dma_start(out=x_sb[g][:], in_=group_rows(x_flat, g))
 
+        w1_bank, w2_bank = {}, {}
         sum_sq, h_rows, h_bank, h_grouped, h_mx, u_bank = {}, {}, {}, {}, {}, {}
         factor, u_squared, act_rows, act_mx, y_bank, yt_bank, z_sb, zt_bank = {}, {}, {}, {}, {}, {}, {}, {}
-        result = {}
+        result, norms, inv_norms = {}, {}, {}
 
         def words(ap, pattern, **sizes):
             return ap.rearrange(pattern, **sizes).bitcast(F32)
 
-        def prepare_w1(c):
+        def tensor_turn_w1(c):
             w1_words = words(w1_rows[:], "p t d -> p (t d)").rearrange("p (t w) -> p t w", t=PACK)
-            w1_out = words(w1_grouped[:], "p c r t -> p (c r t)").rearrange(
-                "p (c r u) -> p c r u", c=PASSES_1, u=2
-            )
             for pair in range(2):
-                bank = psum_b.tile([P, 2, 2 * P], F32)
+                bank = psum_t.tile([P, 2, 2 * P], F32)
                 for u in range(2):
                     for jj in range(2):
                         block = 2 * c + u
@@ -99,29 +105,41 @@ def tile_block_pc_t_kernel(tc, x_mid, wfc, wproj, mlp_scale, out):
                             w1_words[:, 2 * pair + jj, block * P : (block + 1) * P],
                             ident[:],
                         )
-                nc.vector.tensor_copy(
-                    out=w1_out[:, c, pair * 2 * P : (pair + 1) * 2 * P, :],
-                    in_=bank[:].rearrange("p u r -> p r u"),
-                )
+                w1_bank[c, pair] = bank
+
+        def group_w1(c, pair, copy):
+            w1_out = words(w1_grouped[:], "p c r t -> p (c r t)").rearrange(
+                "p (c r u) -> p c r u", c=PASSES_1, u=2
+            )
+            copy(
+                out=w1_out[:, c, pair * 2 * P : (pair + 1) * 2 * P, :],
+                in_=w1_bank[c, pair][:].rearrange("p u r -> p r u"),
+            )
+
+        def quantise_w1(c):
             nc.vector.quantize_mx(
                 out=w1_codes[:, c, :].bitcast(FP8X4),
                 scales=w1_scales[:, c, :],
                 in_=w1_grouped[:, c, :, :].rearrange("p r t -> p (r t)"),
             )
 
-        def prepare_w2(pair):
+        def tensor_turn_w2(pair):
             w2_words = words(w2_rows[:], "p i f -> p (i f)").rearrange(
                 "p (i q u) -> p i q u", i=D_MODEL // P, u=2
             )
-            w2_out = words(w2_grouped[:], "p r t -> p (r t)").rearrange("p (r u) -> p r u", u=2)
-            cols = slice(pair * 2 * P, (pair + 1) * 2 * P)
-            bank = psum_b.tile([P, 2, 2 * P], F32)
+            bank = psum_t.tile([P, 2, 2 * P], F32)
+            warm(bank[:].rearrange("p a b -> p (a b)"), 1)
             for u in range(2):
                 for ii in range(2):
                     nc.tensor.transpose(
                         bank[:, u, ii * P : (ii + 1) * P], w2_words[:, 2 * pair + ii, :, u], ident[:]
                     )
-            nc.vector.tensor_copy(out=w2_out[:, cols, :], in_=bank[:].rearrange("p u r -> p r u"))
+            w2_bank[pair] = bank
+
+        def group_w2(pair, copy):
+            w2_out = words(w2_grouped[:], "p r t -> p (r t)").rearrange("p (r u) -> p r u", u=2)
+            cols = slice(pair * 2 * P, (pair + 1) * 2 * P)
+            copy(out=w2_out[:, cols, :], in_=w2_bank[pair][:].rearrange("p u r -> p r u"))
 
         def quantise_w2(half):
             cols = slice(half * D_MODEL // 2, (half + 1) * D_MODEL // 2)
@@ -131,39 +149,60 @@ def tile_block_pc_t_kernel(tc, x_mid, wfc, wproj, mlp_scale, out):
                 in_=w2_grouped[:, cols, :].rearrange("p r t -> p (r t)"),
             )
 
+        def warm(bank, count):
+            for i in range(count):
+                nc.tensor.matmul(bank, lhsT=zeros[:, 0:P], rhs=zeros[:], start=True, stop=True)
+
+        def first_warm_up():
+            bank = psum_t.tile([P, 2, 2 * P], F32)
+            warm(bank[:].rearrange("p a b -> p (a b)"), 6)
+
+        def widen_gain():
+            nc.vector.tensor_copy(out=gain_rows[:], in_=gain_blocks[:])
+
         def prepare_gain_column():
-            nc.vector.tensor_copy(out=gain_f32[:], in_=gain[:, 0:TURNED])
-            bank = psum_b.tile([P, TURNED_BLOCKS, P], F32)
-            for b in range(TURNED_BLOCKS):
-                nc.tensor.transpose(bank[:, b, :], gain_f32[:, b * P : (b + 1) * P], ident[:])
-            nc.vector.tensor_copy(out=gain_column[:], in_=bank[:, :, 0])
+            bank = psum_t.tile([P, 2, 2 * P], F32)
+            warm(bank[:].rearrange("p a b -> p (a b)"), 1)
+            nc.tensor.transpose(bank[:, 0, 0:P], gain_rows[:], ident[:])
+            nc.vector.tensor_copy(out=gain_column[:], in_=bank[:, 0, 0:TURNED_BLOCKS])
 
 
         def scalar_sum_of_squares(g):
-            n = GROUP_TILES[g]
-            sums = small.tile([P, n], F32)
-            for j in range(n):
-                nc.scalar.activation(
-                    out=squares[:], in_=x_sb[g][:, j, :], func=ACT.Square, accum_out=sums[:, j : j + 1]
-                )
-            norm = small.tile([P, n], F32)
-            nc.scalar.activation(out=norm[:], in_=sums[:], func=ACT.Sqrt, bias=eps[:, 0:1], scale=12.0 / D_MODEL)
-            sum_sq[g] = norm
+            for j in range(GROUP_TILES[g]):
+                sum_tile(g, j)
+
+        def sum_tile(g, j):
+            if j == 0:
+                sums = small.tile([P, GROUP_TILES[g]], F32)
+                sum_sq[g] = sums
+            nc.scalar.activation(
+                out=squares[:], in_=x_sb[g][:, j, :], func=ACT.Square, accum_out=sum_sq[g][:, j : j + 1]
+            )
+
+        def scalar_norm(g):
+            norm = small.tile([P, GROUP_TILES[g]], F32)
+            nc.scalar.activation(
+                out=norm[:], in_=sum_sq[g][:], func=ACT.Sqrt, bias=eps[:, 0:1], scale=12.0 / D_MODEL
+            )
+            norms[g] = norm
+
+        def vector_reciprocal(g):
+            inv_norm = small.tile([P, GROUP_TILES[g]], F32)
+            nc.vector.reciprocal(out=inv_norm[:], in_=norms[g][:])
+            inv_norms[g] = inv_norm
 
         def vector_normalise(g):
             n = GROUP_TILES[g]
-            inv_norm = small.tile([P, n], F32)
-            nc.vector.reciprocal(out=inv_norm[:], in_=sum_sq[g][:])
             h = work.tile([P, n, D_MODEL], BF16)
             for j in range(n):
-                nc.vector.tensor_scalar_mul(out=h[:, j, :], in0=x_sb[g][:, j, :], scalar1=inv_norm[:, j : j + 1])
+                nc.vector.tensor_scalar_mul(out=h[:, j, :], in0=x_sb[g][:, j, :], scalar1=inv_norms[g][:, j : j + 1])
             h_rows[g] = h
 
         def tensor_turn_h(g):
             n = GROUP_TILES[g]
             h_words = words(h_rows[g][:], "p j d -> p (j d)").rearrange("p (j w) -> p j w", j=n)
             for j in range(n):
-                bank = psum_b.tile([P, PASSES_1, 2, P], F32)
+                bank = psum_t.tile([P, PASSES_1, 2, P], F32)
                 for c in range(PASSES_1):
                     for u in range(2):
                         block = 2 * c + u
@@ -209,24 +248,28 @@ def tile_block_pc_t_kernel(tc, x_mid, wfc, wproj, mlp_scale, out):
                         )
                 u_bank[g, j] = bank
 
-        def activate(g):
+        def scalar_square(g):
             n = GROUP_TILES[g]
             sq = work.tile([P, n, P, PACK], BF16)
-            fac = work.tile([P, n, P, PACK], BF16)
             for j in range(n):
-                k = n - 1 - j
                 nc.scalar.activation(
                     out=sq[:, j, :, :], in_=u_bank[g, j][:].rearrange("p t r -> p r t"), func=ACT.Square
                 )
+            u_squared[g] = sq
+
+        def vector_factor(g):
+            n = GROUP_TILES[g]
+            fac = work.tile([P, n, P, PACK], BF16)
+            for j in range(n):
                 nc.vector.tensor_scalar(
-                    out=fac[:, k, :, :],
-                    in0=u_bank[g, k][:].rearrange("p t r -> p r t"),
+                    out=fac[:, j, :, :],
+                    in0=u_bank[g, j][:].rearrange("p t r -> p r t"),
                     scalar1=0.0,
                     scalar2=0.25,
                     op0=ALU.is_ge,
                     op1=ALU.max,
                 )
-            u_squared[g], factor[g] = sq, fac
+            factor[g] = fac
 
         def vector_multiply(g):
             n = GROUP_TILES[g]
@@ -251,7 +294,7 @@ def tile_block_pc_t_kernel(tc, x_mid, wfc, wproj, mlp_scale, out):
             n = GROUP_TILES[g]
             per_bank = BANK // (n * P)
             for first in range(0, TURNED_BLOCKS, per_bank):
-                bank = psum_b.tile([P, per_bank, n * P], F32)
+                bank = psum_t.tile([P, per_bank, n * P], F32)
                 for b in range(first, first + per_bank):
                     channels = slice(b * P, (b + 1) * P)
                     nc.tensor.matmul_mx(
@@ -266,7 +309,7 @@ def tile_block_pc_t_kernel(tc, x_mid, wfc, wproj, mlp_scale, out):
                     yt_bank[g, b] = bank[:, b - first, :]
             for j in range(n):
                 tokens = slice(j * P, (j + 1) * P)
-                bank = psum_a.tile([P, BANK], F32)
+                bank = psum_y.tile([P, BANK], F32)
                 nc.tensor.matmul_mx(
                     out=bank[:],
                     lhsT=codes[:, tokens].bitcast(FP8X4),
@@ -292,7 +335,7 @@ def tile_block_pc_t_kernel(tc, x_mid, wfc, wproj, mlp_scale, out):
             res = results.tile([P, n, D_MODEL], F32)
             for j in range(n):
                 cols = slice(TURNED, D_MODEL)
-                nc.vector.tensor_tensor(out=res[:, j, cols], in0=y_bank[g, j][:], in1=gain[:, cols], op=ALU.mult)
+                nc.vector.tensor_tensor(out=res[:, j, cols], in0=y_bank[g, j][:], in1=gain[:], op=ALU.mult)
                 nc.gpsimd.tensor_tensor(
                     out=res[:, j, cols], in0=res[:, j, cols], in1=x_sb[g][:, j, cols], op=ALU.add
                 )
@@ -300,7 +343,7 @@ def tile_block_pc_t_kernel(tc, x_mid, wfc, wproj, mlp_scale, out):
 
         def tensor_turn_z(g):
             for j in range(GROUP_TILES[g]):
-                bank = psum_a.tile([P, TURNED_BLOCKS, P], F32)
+                bank = psum_t.tile([P, TURNED_BLOCKS, P], F32)
                 for b in range(TURNED_BLOCKS):
                     nc.tensor.transpose(bank[:, b, :], z_sb[g][:, b, j * P : (j + 1) * P], ident[:])
                 zt_bank[g, j] = bank
@@ -315,37 +358,59 @@ def tile_block_pc_t_kernel(tc, x_mid, wfc, wproj, mlp_scale, out):
                 )
             nc.sync.dma_start(out=group_rows(out_flat, g), in_=result[g][:])
 
+        done = set()
+
         def at(stage, g):
-            if 0 <= g < groups:
+            if 0 <= g < groups and (stage, g) not in done:
+                done.add((stage, g))
                 stage(g)
 
+        first_warm_up()
         at(scalar_sum_of_squares, 0)
+        at(scalar_norm, 0)
+        at(vector_reciprocal, 0)
+        at(vector_normalise, 0)
+        at(tensor_turn_h, 0)
         at(scalar_sum_of_squares, 1)
-        for step in range(groups + 7):
-            if step == 2:
-                prepare_w1(0)
-            if step == 3:
-                prepare_w1(1)
-                prepare_w2(0)
-                prepare_w2(1)
-            if step == 4:
-                quantise_w2(0)
-                prepare_w2(2)
-                prepare_w2(3)
-            if step == 5:
-                quantise_w2(1)
-                prepare_gain_column()
-            at(vector_gain, step - 7)
-            at(tensor_output, step - 6)
-            at(vector_finish, step - 7)
+        at(scalar_norm, 1)
+        tensor_turn_w1(0)
+        group_w1(0, 0, nc.vector.tensor_copy)
+        group_w1(0, 1, nc.vector.tensor_copy)
+        at(scalar_group_h, 0)
+        tensor_turn_w1(1)
+        group_w1(1, 0, nc.scalar.copy)
+        group_w1(1, 1, nc.scalar.copy)
+        at(vector_reciprocal, 1)
+        quantise_w1(0)
+        at(vector_normalise, 1)
+        at(vector_quantise_h, 0)
+        quantise_w1(1)
+        at(tensor_turn_h, 1)
+        at(scalar_sum_of_squares, 2)
+        at(scalar_group_h, 1)
+        for step in range(3, groups + 6):
+            at(scalar_square, step - 4)
+            at(scalar_norm, step - 1)
+            at(vector_gain, step - 6)
+            at(tensor_output, step - 5)
+            at(vector_finish, step - 6)
+            at(scalar_gain, step - 5)
             at(tensor_turn_h, step - 2)
-            at(activate, step - 5)
-            at(scalar_gain, step - 6)
-            at(tensor_hidden, step - 4)
+            at(vector_factor, step - 4)
+            at(tensor_turn_z, step - 5)
             at(scalar_group_h, step - 2)
-            at(vector_quantise_h, step - 3)
-            at(tensor_turn_z, step - 6)
-            at(scalar_sum_of_squares, step + 2)
-            at(vector_multiply, step - 5)
+            at(tensor_hidden, step - 3)
+            at(vector_reciprocal, step - 1)
+            at(vector_multiply, step - 4)
+            at(scalar_sum_of_squares, step)
             at(vector_normalise, step - 1)
-            at(vector_quantise_act, step - 5)
+            at(vector_quantise_act, step - 4)
+            at(vector_quantise_h, step - 2)
+            if step == 3:
+                widen_gain()
+                for pair in range(4):
+                    tensor_turn_w2(pair)
+                    group_w2(pair, nc.vector.tensor_copy)
+                quantise_w2(0)
+                prepare_gain_column()
+                quantise_w2(1)

@@ -51,6 +51,7 @@ def tile_block_pc_t_kernel(tc, x_mid, wfc, wproj, mlp_scale, out):
         stack.enter_context(tc.manual_schedule())
 
         ident = keep.tile([P, P], F32)
+        ident_bf16 = keep.tile([P, P], BF16)
         eps = keep.tile([P, 1], F32)
         gain = keep.tile([P, D_MODEL - TURNED], BF16)
         gain_blocks = keep.tile([P, P], BF16)
@@ -67,11 +68,13 @@ def tile_block_pc_t_kernel(tc, x_mid, wfc, wproj, mlp_scale, out):
         w1_grouped = prep.tile([P, PASSES_1, D_FF, PACK], BF16, align_bytes=64)
         w2_grouped = prep.tile([P, D_MODEL, PACK], BF16, align_bytes=64)
         squares = prep.tile([P, D_MODEL], BF16)
+        vector_squares = prep.tile([P, D_MODEL], BF16)
 
         nc.vector.memset(zeros[:], 0.0)
         nc.vector.memset(eps[:], 12.0 * EPS)
         nc.vector.memset(gain_blocks[:], 0.0)
         make_identity(nc, ident[:])
+        make_identity(nc, ident_bf16[:])
         nc.sync.dma_start(out=x_sb[0][:], in_=group_rows(x_flat, 0))
         nc.sync.dma_start(out=x_sb[1][:], in_=group_rows(x_flat, 1))
         nc.sync.dma_start(out=w1_rows[:], in_=wfc.rearrange("(p t) d -> p t d", t=PACK))
@@ -167,17 +170,36 @@ def tile_block_pc_t_kernel(tc, x_mid, wfc, wproj, mlp_scale, out):
             nc.vector.tensor_copy(out=gain_column[:], in_=bank[:, 0, 0:TURNED_BLOCKS])
 
 
+        def on_vector(g, j):
+            return 3 <= g <= 6 and j == 1
+
+        def vector_sum_of_squares(g):
+            sums = small.tile([P, GROUP_TILES[g]], F32)
+            sum_sq[g] = sums
+            for j in range(GROUP_TILES[g]):
+                if on_vector(g, j):
+                    sum_tile(g, j)
+
         def scalar_sum_of_squares(g):
             for j in range(GROUP_TILES[g]):
-                sum_tile(g, j)
+                if not on_vector(g, j):
+                    sum_tile(g, j)
 
         def sum_tile(g, j):
-            if j == 0:
-                sums = small.tile([P, GROUP_TILES[g]], F32)
-                sum_sq[g] = sums
-            nc.scalar.activation(
-                out=squares[:], in_=x_sb[g][:, j, :], func=ACT.Square, accum_out=sum_sq[g][:, j : j + 1]
-            )
+            if on_vector(g, j):
+                nc.vector.scalar_tensor_tensor(
+                    out=vector_squares[:],
+                    in0=x_sb[g][:, j, :],
+                    scalar=1.0,
+                    in1=x_sb[g][:, j, :],
+                    op0=ALU.mult,
+                    op1=ALU.mult,
+                    accum_out=sum_sq[g][:, j : j + 1],
+                )
+            else:
+                nc.scalar.activation(
+                    out=squares[:], in_=x_sb[g][:, j, :], func=ACT.Square, accum_out=sum_sq[g][:, j : j + 1]
+                )
 
         def scalar_norm(g):
             norm = small.tile([P, GROUP_TILES[g]], F32)
@@ -289,7 +311,7 @@ def tile_block_pc_t_kernel(tc, x_mid, wfc, wproj, mlp_scale, out):
             nc.vector.quantize_mx(out=act_codes[:].bitcast(FP8X4), scales=act_scales[:], in_=act_rows[g][:])
             act_mx[g] = (act_codes, act_scales)
 
-        def tensor_output(g):
+        def tensor_turned(g):
             codes, scales = act_mx[g]
             n = GROUP_TILES[g]
             per_bank = BANK // (n * P)
@@ -307,7 +329,10 @@ def tile_block_pc_t_kernel(tc, x_mid, wfc, wproj, mlp_scale, out):
                         stop=True,
                     )
                     yt_bank[g, b] = bank[:, b - first, :]
-            for j in range(n):
+
+        def tensor_direct(g):
+            codes, scales = act_mx[g]
+            for j in range(GROUP_TILES[g]):
                 tokens = slice(j * P, (j + 1) * P)
                 bank = psum_y.tile([P, BANK], F32)
                 nc.tensor.matmul_mx(
@@ -336,7 +361,8 @@ def tile_block_pc_t_kernel(tc, x_mid, wfc, wproj, mlp_scale, out):
             for j in range(n):
                 cols = slice(TURNED, D_MODEL)
                 nc.vector.tensor_tensor(out=res[:, j, cols], in0=y_bank[g, j][:], in1=gain[:], op=ALU.mult)
-                nc.gpsimd.tensor_tensor(
+                adder = nc.vector if g >= groups - 1 else nc.gpsimd
+                adder.tensor_tensor(
                     out=res[:, j, cols], in0=res[:, j, cols], in1=x_sb[g][:, j, cols], op=ALU.add
                 )
             result[g] = res
@@ -344,19 +370,50 @@ def tile_block_pc_t_kernel(tc, x_mid, wfc, wproj, mlp_scale, out):
         def tensor_turn_z(g):
             for j in range(GROUP_TILES[g]):
                 bank = psum_t.tile([P, TURNED_BLOCKS, P], F32)
+                if tensor_adds(g, j):
+                    nc.tensor.matmul(
+                        bank[:].rearrange("p b r -> p (b r)"),
+                        lhsT=ident_bf16[:],
+                        rhs=x_sb[g][:, j, 0:TURNED],
+                        start=True,
+                        stop=False,
+                    )
                 for b in range(TURNED_BLOCKS):
-                    nc.tensor.transpose(bank[:, b, :], z_sb[g][:, b, j * P : (j + 1) * P], ident[:])
+                    turn = z_sb[g][:, b, j * P : (j + 1) * P]
+                    if tensor_adds(g, j):
+                        nc.tensor.matmul(
+                            bank[:, b, :],
+                            lhsT=turn,
+                            rhs=ident[:],
+                            is_transpose=True,
+                            start=False,
+                            stop=(b == TURNED_BLOCKS - 1),
+                        )
+                    else:
+                        nc.tensor.transpose(bank[:, b, :], turn, ident[:])
                 zt_bank[g, j] = bank
+
+        def tensor_adds(g, j):
+            return g >= groups - 7 and j == 0
+
+        def scalar_finish(g):
+            for j in range(GROUP_TILES[g]):
+                if tensor_adds(g, j):
+                    nc.scalar.copy(
+                        out=result[g][:, j, 0:TURNED], in_=zt_bank[g, j][:].rearrange("p b r -> p (b r)")
+                    )
+            nc.sync.dma_start(out=group_rows(out_flat, g), in_=result[g][:])
 
         def vector_finish(g):
             for j in range(GROUP_TILES[g]):
+                if tensor_adds(g, j):
+                    continue
                 nc.vector.tensor_tensor(
                     out=result[g][:, j, 0:TURNED],
                     in0=zt_bank[g, j][:].rearrange("p b r -> p (b r)"),
                     in1=x_sb[g][:, j, 0:TURNED],
                     op=ALU.add,
                 )
-            nc.sync.dma_start(out=group_rows(out_flat, g), in_=result[g][:])
 
         done = set()
 
@@ -366,6 +423,8 @@ def tile_block_pc_t_kernel(tc, x_mid, wfc, wproj, mlp_scale, out):
                 stage(g)
 
         first_warm_up()
+        for g in range(3):
+            at(vector_sum_of_squares, g)
         at(scalar_sum_of_squares, 0)
         at(scalar_norm, 0)
         at(vector_reciprocal, 0)
@@ -389,28 +448,36 @@ def tile_block_pc_t_kernel(tc, x_mid, wfc, wproj, mlp_scale, out):
         at(scalar_sum_of_squares, 2)
         at(scalar_group_h, 1)
         for step in range(3, groups + 6):
+            at(vector_sum_of_squares, step)
             at(scalar_square, step - 4)
             at(scalar_norm, step - 1)
+            if step == 4:
+                group_w2(2, nc.scalar.copy)
+                group_w2(3, nc.scalar.copy)
             at(vector_gain, step - 6)
-            at(tensor_output, step - 5)
+            at(tensor_turned, step - 5)
+            at(tensor_direct, step - 5)
             at(vector_finish, step - 6)
             at(scalar_gain, step - 5)
             at(tensor_turn_h, step - 2)
             at(vector_factor, step - 4)
-            at(tensor_turn_z, step - 5)
             at(scalar_group_h, step - 2)
             at(tensor_hidden, step - 3)
+            at(tensor_turn_z, step - 5)
             at(vector_reciprocal, step - 1)
             at(vector_multiply, step - 4)
+            at(scalar_finish, step - 6)
             at(scalar_sum_of_squares, step)
             at(vector_normalise, step - 1)
+            if step == 4:
+                quantise_w2(1)
             at(vector_quantise_act, step - 4)
             at(vector_quantise_h, step - 2)
             if step == 3:
                 widen_gain()
                 for pair in range(4):
                     tensor_turn_w2(pair)
-                    group_w2(pair, nc.vector.tensor_copy)
+                    if pair < 2:
+                        group_w2(pair, nc.vector.tensor_copy)
                 quantise_w2(0)
                 prepare_gain_column()
-                quantise_w2(1)

@@ -171,7 +171,7 @@ def tile_block_pc_t_kernel(tc, x_mid, wfc, wproj, mlp_scale, out):
 
 
         def on_vector(g, j):
-            return 3 <= g <= 6 and j == 1
+            return g in (3, 5, 6) and j == 1
 
         def vector_sum_of_squares(g):
             sums = small.tile([P, GROUP_TILES[g]], F32)
@@ -202,15 +202,14 @@ def tile_block_pc_t_kernel(tc, x_mid, wfc, wproj, mlp_scale, out):
                 )
 
         def scalar_norm(g):
-            norm = small.tile([P, GROUP_TILES[g]], F32)
-            nc.scalar.activation(
-                out=norm[:], in_=sum_sq[g][:], func=ACT.Sqrt, bias=eps[:, 0:1], scale=12.0 / D_MODEL
-            )
-            norms[g] = norm
-
-        def vector_reciprocal(g):
             inv_norm = small.tile([P, GROUP_TILES[g]], F32)
-            nc.vector.reciprocal(out=inv_norm[:], in_=norms[g][:])
+            nc.scalar.activation(
+                out=inv_norm[:],
+                in_=sum_sq[g][:],
+                func=ACT.Abs_reciprocal_sqrt,
+                bias=eps[:, 0:1],
+                scale=12.0 / D_MODEL,
+            )
             inv_norms[g] = inv_norm
 
         def vector_normalise(g):
@@ -225,6 +224,8 @@ def tile_block_pc_t_kernel(tc, x_mid, wfc, wproj, mlp_scale, out):
             h_words = words(h_rows[g][:], "p j d -> p (j d)").rearrange("p (j w) -> p j w", j=n)
             for j in range(n):
                 bank = psum_t.tile([P, PASSES_1, 2, P], F32)
+                if g == 1:
+                    warm(bank[:].rearrange("p c u r -> p (c u r)"), 4)
                 for c in range(PASSES_1):
                     for u in range(2):
                         block = 2 * c + u
@@ -427,7 +428,6 @@ def tile_block_pc_t_kernel(tc, x_mid, wfc, wproj, mlp_scale, out):
             at(vector_sum_of_squares, g)
         at(scalar_sum_of_squares, 0)
         at(scalar_norm, 0)
-        at(vector_reciprocal, 0)
         at(vector_normalise, 0)
         at(tensor_turn_h, 0)
         at(scalar_sum_of_squares, 1)
@@ -439,7 +439,6 @@ def tile_block_pc_t_kernel(tc, x_mid, wfc, wproj, mlp_scale, out):
         tensor_turn_w1(1)
         group_w1(1, 0, nc.scalar.copy)
         group_w1(1, 1, nc.scalar.copy)
-        at(vector_reciprocal, 1)
         quantise_w1(0)
         at(vector_normalise, 1)
         at(vector_quantise_h, 0)
@@ -464,7 +463,6 @@ def tile_block_pc_t_kernel(tc, x_mid, wfc, wproj, mlp_scale, out):
             at(scalar_group_h, step - 2)
             at(tensor_hidden, step - 3)
             at(tensor_turn_z, step - 5)
-            at(vector_reciprocal, step - 1)
             at(vector_multiply, step - 4)
             at(scalar_finish, step - 6)
             at(scalar_sum_of_squares, step)

@@ -350,11 +350,20 @@ def tile_block_pc_t_kernel(tc, x_mid, wfc, wproj, mlp_scale, out):
         def scalar_gain(g):
             n = GROUP_TILES[g]
             z = work.tile([P, TURNED_BLOCKS, n * P], F32)
-            for b in range(TURNED_BLOCKS):
+            z_sb[g] = z
+            for b in range(TURNED_BLOCKS - vector_blocks(g)):
                 nc.scalar.activation(
                     out=z[:, b, :], in_=yt_bank[g, b], func=ACT.Copy, scale=gain_column[:, b : b + 1]
                 )
-            z_sb[g] = z
+
+        def vector_blocks(g):
+            return 1 if g % 2 == 0 and g < groups - 5 else 0
+
+        def vector_gain_turned(g):
+            for b in range(TURNED_BLOCKS - vector_blocks(g), TURNED_BLOCKS):
+                nc.vector.tensor_scalar_mul(
+                    out=z_sb[g][:, b, :], in0=yt_bank[g, b], scalar1=gain_column[:, b : b + 1]
+                )
 
         def vector_gain(g):
             n = GROUP_TILES[g]
@@ -395,7 +404,7 @@ def tile_block_pc_t_kernel(tc, x_mid, wfc, wproj, mlp_scale, out):
                 zt_bank[g, j] = bank
 
         def tensor_adds(g, j):
-            return g >= groups - 7 and j == 0
+            return g >= groups - 8 and j == 0
 
         def scalar_finish(g):
             for j in range(GROUP_TILES[g]):
@@ -460,6 +469,7 @@ def tile_block_pc_t_kernel(tc, x_mid, wfc, wproj, mlp_scale, out):
             at(scalar_gain, step - 5)
             at(tensor_turn_h, step - 2)
             at(vector_factor, step - 4)
+            at(vector_gain_turned, step - 5)
             at(scalar_group_h, step - 2)
             at(tensor_hidden, step - 3)
             at(tensor_turn_z, step - 5)

@@ -371,11 +371,28 @@ def tile_block_pc_t_kernel(tc, x_mid, wfc, wproj, mlp_scale, out):
             for j in range(n):
                 cols = slice(TURNED, D_MODEL)
                 nc.vector.tensor_tensor(out=res[:, j, cols], in0=y_bank[g, j][:], in1=gain[:], op=ALU.mult)
-                adder = nc.vector if g >= groups - 1 else nc.gpsimd
-                adder.tensor_tensor(
-                    out=res[:, j, cols], in0=res[:, j, cols], in1=x_sb[g][:, j, cols], op=ALU.add
-                )
+                if not vector_adds(g, j):
+                    add_direct(nc.gpsimd, res, g, j)
             result[g] = res
+
+        def vector_adds(g, j):
+            return g >= groups - 2 or g >= groups - 4 and j == 1
+
+        def add_direct(engine, res, g, j):
+            cols = slice(TURNED, D_MODEL)
+            engine.tensor_tensor(out=res[:, j, cols], in0=res[:, j, cols], in1=x_sb[g][:, j, cols], op=ALU.add)
+
+        def vector_add(g):
+            for j in range(GROUP_TILES[g]):
+                if vector_adds(g, j):
+                    add_direct(nc.vector, result[g], g, j)
+            store(g, slice(TURNED, D_MODEL) if in_halves(g) else slice(0, D_MODEL))
+
+        def in_halves(g):
+            return g >= groups - 3
+
+        def store(g, cols):
+            nc.sync.dma_start(out=group_rows(out_flat, g)[:, :, cols], in_=result[g][:, :, cols])
 
         def tensor_turn_z(g):
             for j in range(GROUP_TILES[g]):
@@ -404,7 +421,7 @@ def tile_block_pc_t_kernel(tc, x_mid, wfc, wproj, mlp_scale, out):
                 zt_bank[g, j] = bank
 
         def tensor_adds(g, j):
-            return g >= groups - 8 and j == 0
+            return g >= groups - 4 or g >= groups - 8 and j == 0
 
         def scalar_finish(g):
             for j in range(GROUP_TILES[g]):
@@ -412,7 +429,8 @@ def tile_block_pc_t_kernel(tc, x_mid, wfc, wproj, mlp_scale, out):
                     nc.scalar.copy(
                         out=result[g][:, j, 0:TURNED], in_=zt_bank[g, j][:].rearrange("p b r -> p (b r)")
                     )
-            nc.sync.dma_start(out=group_rows(out_flat, g), in_=result[g][:])
+            if in_halves(g):
+                store(g, slice(0, TURNED))
 
         def vector_finish(g):
             for j in range(GROUP_TILES[g]):
@@ -481,6 +499,7 @@ def tile_block_pc_t_kernel(tc, x_mid, wfc, wproj, mlp_scale, out):
                 quantise_w2(1)
             at(vector_quantise_act, step - 4)
             at(vector_quantise_h, step - 2)
+            at(vector_add, step - 6)
             if step == 3:
                 widen_gain()
                 for pair in range(4):

@@ -19,6 +19,7 @@ D_MODEL = 1024
 D_FF = 512
 EPS = 1e-6
 PASSES_1 = D_MODEL // K_PASS
+COLUMNS = 4
 BANK = 512
 TURNED = 512
 TURNED_BLOCKS = TURNED // P
@@ -95,6 +96,9 @@ def tile_block_pc_t_kernel(tc, x_mid, wfc, wproj, mlp_scale, out):
 
         def words(ap, pattern, **sizes):
             return ap.rearrange(pattern, **sizes).bitcast(F32)
+
+        def by_columns(ap):
+            return ap.rearrange("p (c i) t -> p c t i", i=COLUMNS)
 
         def tensor_turn_w1(c):
             w1_words = words(w1_rows[:], "p t d -> p (t d)").rearrange("p (t w) -> p t w", t=PACK)
@@ -276,7 +280,9 @@ def tile_block_pc_t_kernel(tc, x_mid, wfc, wproj, mlp_scale, out):
             sq = work.tile([P, n, P, PACK], BF16)
             for j in range(n):
                 nc.scalar.activation(
-                    out=sq[:, j, :, :], in_=u_bank[g, j][:].rearrange("p t r -> p r t"), func=ACT.Square
+                    out=by_columns(sq[:, j, :, :]),
+                    in_=u_bank[g, j][:].rearrange("p t (c i) -> p c t i", i=COLUMNS),
+                    func=ACT.Square,
                 )
             u_squared[g] = sq
 
@@ -285,8 +291,8 @@ def tile_block_pc_t_kernel(tc, x_mid, wfc, wproj, mlp_scale, out):
             fac = work.tile([P, n, P, PACK], BF16)
             for j in range(n):
                 nc.vector.tensor_scalar(
-                    out=fac[:, j, :, :],
-                    in0=u_bank[g, j][:].rearrange("p t r -> p r t"),
+                    out=by_columns(fac[:, j, :, :]),
+                    in0=u_bank[g, j][:].rearrange("p t (c i) -> p c t i", i=COLUMNS),
                     scalar1=0.0,
                     scalar2=0.25,
                     op0=ALU.is_ge,

from contextlib import ExitStack

import concourse.mybir as mybir
from concourse.masks import make_identity

F32 = mybir.dt.float32
BF16 = mybir.dt.bfloat16
U32 = mybir.dt.uint32
U8 = mybir.dt.uint8
FP8X4 = mybir.dt.float8_e4m3fn_x4
ACT = mybir.ActivationFunctionType
ALU = mybir.AluOpType

P = 128
PACK = 4
K_PASS = P * PACK
TOKENS = 4096
D_MODEL = 1024
D_FF = 512
EPS = 1e-6
PASSES_1 = D_MODEL // K_PASS
COLUMNS = 4
BANK = 512
TURNED = 512
TURNED_BLOCKS = TURNED // P

GROUP_TILES = [1, 1] + [2] * 14 + [1, 1]

FLOPS = 2 * TOKENS * D_MODEL * D_FF * 2


def tile_block_pc_t_kernel(tc, x_mid, wfc, wproj, mlp_scale, out):
    nc = tc.nc
    x_flat = x_mid.flatten_outer_dims()
    out_flat = out.flatten_outer_dims()
    groups = len(GROUP_TILES)

    def group_rows(flat, g):
        n = GROUP_TILES[g]
        first = sum(GROUP_TILES[:g]) * P
        return flat[first : first + n * P, :].rearrange("(p j) d -> p j d", j=n)

    with ExitStack() as stack:
        keep = stack.enter_context(tc.tile_pool(name="keep", bufs=1))
        psum_y = stack.enter_context(tc.psum_pool(name="psum_y", bufs=2))
        psum_t = stack.enter_context(tc.psum_pool(name="psum_t", bufs=4))
        psum_u = stack.enter_context(tc.psum_pool(name="psum_u", bufs=2))
        prep = stack.enter_context(tc.tile_pool(name="prep", bufs=1))
        work = stack.enter_context(tc.tile_pool(name="work", bufs=3))
        small = stack.enter_context(tc.tile_pool(name="small", bufs=8))
        results = stack.enter_context(tc.tile_pool(name="results", bufs=4))
        stack.enter_context(tc.manual_schedule())

        ident = keep.tile([P, P], F32)
        ident_bf16 = keep.tile([P, P], BF16)
        eps = keep.tile([P, 1], F32)
        gain = keep.tile([P, D_MODEL - TURNED], BF16)
        gain_blocks = keep.tile([P, P], BF16)
        gain_rows = keep.tile([P, P], F32)
        zeros = keep.tile([P, BANK], BF16)
        gain_column = keep.tile([P, TURNED_BLOCKS], F32)
        x_sb = [keep.tile([P, GROUP_TILES[g], D_MODEL], BF16, name="x%d" % g) for g in range(groups)]
        w1_codes = keep.tile([P, PASSES_1, D_FF], U32, align_bytes=64)
        w1_scales = keep.tile([P, PASSES_1, D_FF], U8, align_bytes=64)
        w2_codes = keep.tile([P, D_MODEL], U32, align_bytes=64)
        w2_scales = keep.tile([P, D_MODEL], U8, align_bytes=64)
        w1_rows = prep.tile([P, PACK, D_MODEL], BF16)
        w2_rows = prep.tile([P, D_MODEL // P, D_FF], BF16)
        w1_grouped = prep.tile([P, PASSES_1, D_FF, PACK], BF16, align_bytes=64)
        w2_grouped = prep.tile([P, D_MODEL, PACK], BF16, align_bytes=64)
        squares = prep.tile([P, D_MODEL], BF16)
        vector_squares = prep.tile([P, D_MODEL], BF16)

        nc.vector.memset(zeros[:], 0.0)
        nc.vector.memset(eps[:], 12.0 * EPS)
        nc.vector.memset(gain_blocks[:], 0.0)
        make_identity(nc, ident[:])
        make_identity(nc, ident_bf16[:])
        nc.sync.dma_start(out=x_sb[0][:], in_=group_rows(x_flat, 0))
        nc.sync.dma_start(out=x_sb[1][:], in_=group_rows(x_flat, 1))
        nc.sync.dma_start(out=w1_rows[:], in_=wfc.rearrange("(p t) d -> p t d", t=PACK))
        nc.sync.dma_start(out=x_sb[2][:], in_=group_rows(x_flat, 2))
        nc.sync.dma_start(out=w2_rows[:], in_=wproj.rearrange("(i r) f -> r i f", r=P))
        nc.sync.dma_start(
            out=gain_blocks[0:TURNED_BLOCKS, :], in_=mlp_scale[0:TURNED].rearrange("(b c) -> b c", c=P)
        )
        nc.sync.dma_start(out=x_sb[3][:], in_=group_rows(x_flat, 3))
        nc.sync.dma_start(out=gain[:], in_=mlp_scale[TURNED:D_MODEL].partition_broadcast(P))
        for g in range(4, groups):
            nc.sync.dma_start(out=x_sb[g][:], in_=group_rows(x_flat, g))

        w1_bank, w2_bank = {}, {}
        sum_sq, h_rows, h_bank, h_grouped, h_mx, u_bank = {}, {}, {}, {}, {}, {}
        factor, u_squared, act_rows, act_mx, y_bank, yt_bank, z_sb, zt_bank = {}, {}, {}, {}, {}, {}, {}, {}
        result, norms, inv_norms = {}, {}, {}

        def words(ap, pattern, **sizes):
            return ap.rearrange(pattern, **sizes).bitcast(F32)

        def by_columns(ap):
            return ap.rearrange("p (c i) t -> p c t i", i=COLUMNS)

        def tensor_turn_w1(c):
            w1_words = words(w1_rows[:], "p t d -> p (t d)").rearrange("p (t w) -> p t w", t=PACK)
            for pair in range(2):
                bank = psum_t.tile([P, 2, 2 * P], F32)
                for u in range(2):
                    for jj in range(2):
                        block = 2 * c + u
                        nc.tensor.transpose(
                            bank[:, u, jj * P : (jj + 1) * P],
                            w1_words[:, 2 * pair + jj, block * P : (block + 1) * P],
                            ident[:],
                        )
                w1_bank[c, pair] = bank

        def group_w1(c, pair, copy):
            w1_out = words(w1_grouped[:], "p c r t -> p (c r t)").rearrange(
                "p (c r u) -> p c r u", c=PASSES_1, u=2
            )
            copy(
                out=w1_out[:, c, pair * 2 * P : (pair + 1) * 2 * P, :],
                in_=w1_bank[c, pair][:].rearrange("p u r -> p r u"),
            )

        def quantise_w1(c):
            nc.vector.quantize_mx(
                out=w1_codes[:, c, :].bitcast(FP8X4),
                scales=w1_scales[:, c, :],
                in_=w1_grouped[:, c, :, :].rearrange("p r t -> p (r t)"),
            )

        def tensor_turn_w2(pair):
            w2_words = words(w2_rows[:], "p i f -> p (i f)").rearrange(
                "p (i q u) -> p i q u", i=D_MODEL // P, u=2
            )
            bank = psum_t.tile([P, 2, 2 * P], F32)
            warm(bank[:].rearrange("p a b -> p (a b)"), 1)
            for u in range(2):
                for ii in range(2):
                    nc.tensor.transpose(
                        bank[:, u, ii * P : (ii + 1) * P], w2_words[:, 2 * pair + ii, :, u], ident[:]
                    )
            w2_bank[pair] = bank

        def group_w2(pair, copy):
            w2_out = words(w2_grouped[:], "p r t -> p (r t)").rearrange("p (r u) -> p r u", u=2)
            cols = slice(pair * 2 * P, (pair + 1) * 2 * P)
            copy(out=w2_out[:, cols, :], in_=w2_bank[pair][:].rearrange("p u r -> p r u"))

        def quantise_w2(half):
            cols = slice(half * D_MODEL // 2, (half + 1) * D_MODEL // 2)
            nc.vector.quantize_mx(
                out=w2_codes[:, cols].bitcast(FP8X4),
                scales=w2_scales[:, cols],
                in_=w2_grouped[:, cols, :].rearrange("p r t -> p (r t)"),
            )

        def warm(bank, count):
            for i in range(count):
                nc.tensor.matmul(bank, lhsT=zeros[:, 0:P], rhs=zeros[:], start=True, stop=True)

        def first_warm_up():
            bank = psum_t.tile([P, 2, 2 * P], F32)
            warm(bank[:].rearrange("p a b -> p (a b)"), 6)

        def widen_gain():
            nc.vector.tensor_copy(out=gain_rows[:], in_=gain_blocks[:])

        def prepare_gain_column():
            bank = psum_t.tile([P, 2, 2 * P], F32)
            warm(bank[:].rearrange("p a b -> p (a b)"), 1)
            nc.tensor.transpose(bank[:, 0, 0:P], gain_rows[:], ident[:])
            nc.vector.tensor_copy(out=gain_column[:], in_=bank[:, 0, 0:TURNED_BLOCKS])


        def on_vector(g, j):
            return g in (3, 5, 6) and j == 1

        def vector_sum_of_squares(g):
            sums = small.tile([P, GROUP_TILES[g]], F32)
            sum_sq[g] = sums
            for j in range(GROUP_TILES[g]):
                if on_vector(g, j):
                    sum_tile(g, j)

        def scalar_sum_of_squares(g):
            for j in range(GROUP_TILES[g]):
                if not on_vector(g, j):
                    sum_tile(g, j)

        def sum_tile(g, j):
            if on_vector(g, j):
                nc.vector.scalar_tensor_tensor(
                    out=vector_squares[:],
                    in0=x_sb[g][:, j, :],
                    scalar=1.0,
                    in1=x_sb[g][:, j, :],
                    op0=ALU.mult,
                    op1=ALU.mult,
                    accum_out=sum_sq[g][:, j : j + 1],
                )
            else:
                nc.scalar.activation(
                    out=squares[:], in_=x_sb[g][:, j, :], func=ACT.Square, accum_out=sum_sq[g][:, j : j + 1]
                )

        def scalar_norm(g):
            inv_norm = small.tile([P, GROUP_TILES[g]], F32)
            nc.scalar.activation(
                out=inv_norm[:],
                in_=sum_sq[g][:],
                func=ACT.Abs_reciprocal_sqrt,
                bias=eps[:, 0:1],
                scale=12.0 / D_MODEL,
            )
            inv_norms[g] = inv_norm

        def vector_normalise(g):
            n = GROUP_TILES[g]
            h = work.tile([P, n, D_MODEL], BF16)
            for j in range(n):
                nc.vector.tensor_scalar_mul(out=h[:, j, :], in0=x_sb[g][:, j, :], scalar1=inv_norms[g][:, j : j + 1])
            h_rows[g] = h

        def tensor_turn_h(g):
            n = GROUP_TILES[g]
            h_words = words(h_rows[g][:], "p j d -> p (j d)").rearrange("p (j w) -> p j w", j=n)
            for j in range(n):
                bank = psum_t.tile([P, PASSES_1, 2, P], F32)
                if g == 1:
                    warm(bank[:].rearrange("p c u r -> p (c u r)"), 4)
                for c in range(PASSES_1):
                    for u in range(2):
                        block = 2 * c + u
                        nc.tensor.transpose(bank[:, c, u, :], h_words[:, j, block * P : (block + 1) * P], ident[:])
                h_bank[g, j] = bank

        def scalar_group_h(g):
            n = GROUP_TILES[g]
            grouped = work.tile([P, n, PASSES_1, P, PACK], BF16, align_bytes=64)
            grouped_words = words(grouped[:], "p j c r t -> p (j c r t)").rearrange(
                "p (j c r u) -> p j c r u", j=n, c=PASSES_1, u=2
            )
            for j in range(n):
                nc.scalar.copy(out=grouped_words[:, j], in_=h_bank[g, j][:].rearrange("p c u r -> p c r u"))
            h_grouped[g] = grouped

        def vector_quantise_h(g):
            n = GROUP_TILES[g]
            h_codes = work.tile([P, n, PASSES_1, P], U32, align_bytes=64)
            h_scales = work.tile([P, n, PASSES_1, P], U8, align_bytes=64)
            nc.vector.quantize_mx(
                out=h_codes[:].rearrange("p j c r -> p (j c r)").bitcast(FP8X4),
                scales=h_scales[:].rearrange("p j c r -> p (j c r)"),
                in_=h_grouped[g][:].rearrange("p j c r t -> p (j c r t)"),
            )
            h_mx[g] = (h_codes, h_scales)

        def tensor_hidden(g):
            codes, scales = h_mx[g]
            for j in range(GROUP_TILES[g]):
                bank = psum_u.tile([P, PACK, P], F32)
                for t in range(PACK):
                    rows = slice(t * P, (t + 1) * P)
                    for c in range(PASSES_1):
                        nc.tensor.matmul_mx(
                            out=bank[:, t, :],
                            lhsT=w1_codes[:, c, rows].bitcast(FP8X4),
                            lhsT_scale=w1_scales[:, c, rows],
                            rhs=codes[:, j, c, :].bitcast(FP8X4),
                            rhs_scale=scales[:, j, c, :],
                            start=(c == 0),
                            stop=(c == PASSES_1 - 1),
                        )
                u_bank[g, j] = bank

        def scalar_square(g):
            n = GROUP_TILES[g]
            sq = work.tile([P, n, P, PACK], BF16)
            for j in range(n):
                nc.scalar.activation(
                    out=by_columns(sq[:, j, :, :]),
                    in_=u_bank[g, j][:].rearrange("p t (c i) -> p c t i", i=COLUMNS),
                    func=ACT.Square,
                )
            u_squared[g] = sq

        def vector_factor(g):
            n = GROUP_TILES[g]
            fac = work.tile([P, n, P, PACK], BF16)
            for j in range(n):
                nc.vector.tensor_scalar(
                    out=by_columns(fac[:, j, :, :]),
                    in0=u_bank[g, j][:].rearrange("p t (c i) -> p c t i", i=COLUMNS),
                    scalar1=0.0,
                    scalar2=0.25,
                    op0=ALU.is_ge,
                    op1=ALU.max,
                )
            factor[g] = fac

        def vector_multiply(g):
            n = GROUP_TILES[g]
            act = work.tile([P, n * P * PACK], BF16, align_bytes=64)
            nc.vector.tensor_tensor(
                out=act[:],
                in0=u_squared[g][:].rearrange("p j r t -> p (j r t)"),
                in1=factor[g][:].rearrange("p j r t -> p (j r t)"),
                op=ALU.mult,
            )
            act_rows[g] = act

        def vector_quantise_act(g):
            n = GROUP_TILES[g]
            act_codes = work.tile([P, n * P], U32, align_bytes=64)
            act_scales = work.tile([P, n * P], U8, align_bytes=64)
            nc.vector.quantize_mx(out=act_codes[:].bitcast(FP8X4), scales=act_scales[:], in_=act_rows[g][:])
            act_mx[g] = (act_codes, act_scales)

        def tensor_turned(g):
            codes, scales = act_mx[g]
            n = GROUP_TILES[g]
            per_bank = BANK // (n * P)
            for first in range(0, TURNED_BLOCKS, per_bank):
                bank = psum_t.tile([P, per_bank, n * P], F32)
                for b in range(first, first + per_bank):
                    channels = slice(b * P, (b + 1) * P)
                    nc.tensor.matmul_mx(
                        out=bank[:, b - first, :],
                        lhsT=w2_codes[:, channels].bitcast(FP8X4),
                        lhsT_scale=w2_scales[:, channels],
                        rhs=codes[:].bitcast(FP8X4),
                        rhs_scale=scales[:],
                        start=True,
                        stop=True,
                    )
                    yt_bank[g, b] = bank[:, b - first, :]

        def tensor_direct(g):
            codes, scales = act_mx[g]
            for j in range(GROUP_TILES[g]):
                tokens = slice(j * P, (j + 1) * P)
                bank = psum_y.tile([P, BANK], F32)
                nc.tensor.matmul_mx(
                    out=bank[:],
                    lhsT=codes[:, tokens].bitcast(FP8X4),
                    lhsT_scale=scales[:, tokens],
                    rhs=w2_codes[:, TURNED:D_MODEL].bitcast(FP8X4),
                    rhs_scale=w2_scales[:, TURNED:D_MODEL],
                    start=True,
                    stop=True,
                )
                y_bank[g, j] = bank

        def scalar_gain(g):
            n = GROUP_TILES[g]
            z = work.tile([P, TURNED_BLOCKS, n * P], F32)
            z_sb[g] = z
            for b in range(TURNED_BLOCKS - vector_blocks(g)):
                nc.scalar.activation(
                    out=z[:, b, :], in_=yt_bank[g, b], func=ACT.Copy, scale=gain_column[:, b : b + 1]
                )

        def vector_blocks(g):
            return 1 if g % 2 == 0 and g < groups - 5 else 0

        def vector_gain_turned(g):
            for b in range(TURNED_BLOCKS - vector_blocks(g), TURNED_BLOCKS):
                nc.vector.tensor_scalar_mul(
                    out=z_sb[g][:, b, :], in0=yt_bank[g, b], scalar1=gain_column[:, b : b + 1]
                )

        def vector_gain(g):
            n = GROUP_TILES[g]
            res = results.tile([P, n, D_MODEL], F32)
            for j in range(n):
                cols = slice(TURNED, D_MODEL)
                nc.vector.tensor_tensor(out=res[:, j, cols], in0=y_bank[g, j][:], in1=gain[:], op=ALU.mult)
                if not vector_adds(g, j):
                    add_direct(nc.gpsimd, res, g, j)
            result[g] = res

        def vector_adds(g, j):
            return g >= groups - 2 or g >= groups - 4 and j == 1

        def add_direct(engine, res, g, j):
            cols = slice(TURNED, D_MODEL)
            engine.tensor_tensor(out=res[:, j, cols], in0=res[:, j, cols], in1=x_sb[g][:, j, cols], op=ALU.add)

        def vector_add(g):
            for j in range(GROUP_TILES[g]):
                if vector_adds(g, j):
                    add_direct(nc.vector, result[g], g, j)
            store(g, slice(TURNED, D_MODEL) if in_halves(g) else slice(0, D_MODEL))

        def in_halves(g):
            return g >= groups - 3

        def store(g, cols):
            nc.sync.dma_start(out=group_rows(out_flat, g)[:, :, cols], in_=result[g][:, :, cols])

        def tensor_turn_z(g):
            for j in range(GROUP_TILES[g]):
                bank = psum_t.tile([P, TURNED_BLOCKS, P], F32)
                if tensor_adds(g, j):
                    nc.tensor.matmul(
                        bank[:].rearrange("p b r -> p (b r)"),
                        lhsT=ident_bf16[:],
                        rhs=x_sb[g][:, j, 0:TURNED],
                        start=True,
                        stop=False,
                    )
                for b in range(TURNED_BLOCKS):
                    turn = z_sb[g][:, b, j * P : (j + 1) * P]
                    if tensor_adds(g, j):
                        nc.tensor.matmul(
                            bank[:, b, :],
                            lhsT=turn,
                            rhs=ident[:],
                            is_transpose=True,
                            start=False,
                            stop=(b == TURNED_BLOCKS - 1),
                        )
                    else:
                        nc.tensor.transpose(bank[:, b, :], turn, ident[:])
                zt_bank[g, j] = bank

        def tensor_adds(g, j):
            return g >= groups - 4 or g >= groups - 8 and j == 0

        def scalar_finish(g):
            for j in range(GROUP_TILES[g]):
                if tensor_adds(g, j):
                    nc.scalar.copy(
                        out=result[g][:, j, 0:TURNED], in_=zt_bank[g, j][:].rearrange("p b r -> p (b r)")
                    )
            if in_halves(g):
                store(g, slice(0, TURNED))

        def vector_finish(g):
            for j in range(GROUP_TILES[g]):
                if tensor_adds(g, j):
                    continue
                nc.vector.tensor_tensor(
                    out=result[g][:, j, 0:TURNED],
                    in0=zt_bank[g, j][:].rearrange("p b r -> p (b r)"),
                    in1=x_sb[g][:, j, 0:TURNED],
                    op=ALU.add,
                )

        done = set()

        def at(stage, g):
            if 0 <= g < groups and (stage, g) not in done:
                done.add((stage, g))
                stage(g)

        first_warm_up()
        for g in range(3):
            at(vector_sum_of_squares, g)
        at(scalar_sum_of_squares, 0)
        at(scalar_norm, 0)
        at(vector_normalise, 0)
        at(tensor_turn_h, 0)
        at(scalar_sum_of_squares, 1)
        at(scalar_norm, 1)
        tensor_turn_w1(0)
        group_w1(0, 0, nc.vector.tensor_copy)
        group_w1(0, 1, nc.vector.tensor_copy)
        at(scalar_group_h, 0)
        tensor_turn_w1(1)
        group_w1(1, 0, nc.scalar.copy)
        group_w1(1, 1, nc.scalar.copy)
        quantise_w1(0)
        at(vector_normalise, 1)
        at(vector_quantise_h, 0)
        quantise_w1(1)
        at(tensor_turn_h, 1)
        at(scalar_sum_of_squares, 2)
        at(scalar_group_h, 1)
        for step in range(3, groups + 6):
            at(vector_sum_of_squares, step)
            at(scalar_square, step - 4)
            at(scalar_norm, step - 1)
            if step == 4:
                group_w2(2, nc.scalar.copy)
                group_w2(3, nc.scalar.copy)
            at(vector_gain, step - 6)
            at(tensor_turned, step - 5)
            at(tensor_direct, step - 5)
            at(vector_finish, step - 6)
            at(scalar_gain, step - 5)
            at(tensor_turn_h, step - 2)
            at(vector_factor, step - 4)
            at(vector_gain_turned, step - 5)
            at(scalar_group_h, step - 2)
            at(tensor_hidden, step - 3)
            at(tensor_turn_z, step - 5)
            at(vector_multiply, step - 4)
            at(scalar_finish, step - 6)
            at(scalar_sum_of_squares, step)
            at(vector_normalise, step - 1)
            if step == 4:
                quantise_w2(1)
            at(vector_quantise_act, step - 4)
            at(vector_quantise_h, step - 2)
            at(vector_add, step - 6)
            if step == 3:
                widen_gain()
                for pair in range(4):
                    tensor_turn_w2(pair)
                    if pair < 2:
                        group_w2(pair, nc.vector.tensor_copy)
                quantise_w2(0)
                prepare_gain_column()
